import numpy as np
import ml_dtypes


def mxq(x, axis, fmt="e4m3"):
    dtype, down = {"e4m3": (ml_dtypes.float8_e4m3fn, 7), "e5m2": (ml_dtypes.float8_e5m2, 14)}[fmt]
    v = np.moveaxis(np.asarray(x, np.float32).astype(ml_dtypes.bfloat16).astype(np.float64), axis, -1)
    blocks = v.reshape(v.shape[:-1] + (-1, 32))
    amax = np.abs(blocks).max(-1, keepdims=True)
    byte = np.maximum(np.where(amax > 0, np.frexp(amax)[1] - 1 + 127, 0) - down, 1)
    scale = np.exp2(byte - 127.0)
    codes = (blocks / scale).astype(np.float32).astype(dtype).astype(np.float64)
    return np.moveaxis((codes * scale).reshape(v.shape), -1, axis)


WIDE = False


def mx_kscale(k):
    if not WIDE:
        return np.ones(k)
    levels = np.array([10, -10, 5, -5, 0])
    if k % 512:
        return np.exp2(np.random.permutation(np.resize(levels, k // 32))).repeat(32)
    a = np.empty((k // 512, 16))
    for p in range(k // 512):
        a[p, :8] = np.random.permutation(np.resize(levels, 8))
        for g in range(8):
            far = levels[np.abs(levels - a[p, g]) >= 10]
            a[p, g + 8] = far[np.random.randint(len(far))]
    return np.exp2(a.ravel()).repeat(32)


BF16 = ml_dtypes.bfloat16


def bf(x):
    return np.asarray(x, np.float32).astype(BF16)


def f64(x):
    return np.asarray(x).astype(np.float64)


B, T, D, NH, N_MLP = 4, 128, 1024, 16, 4096
HD = D // NH
LN_EPS = 1e-6


def layer_norm(v, g, b):
    mu = v.mean(-1, keepdims=True)
    var = np.square(v - mu).mean(-1, keepdims=True)
    return (v - mu) / np.sqrt(var + LN_EPS) * g + b


def setup_inputs():
    s = mx_kscale(D)
    return {"x": bf(np.random.standard_normal((B, T, D)) * 1.5 + np.random.standard_normal((B, T, 1)) * 0.5),
            "W_qkv": bf(np.random.standard_normal((3 * D, D)) / np.sqrt(D) / s),
            "b_qkv": bf(np.random.standard_normal(3 * D) * 0.2),
            "g1": bf((1.0 + 0.1 * np.random.standard_normal(D)) * s),
            "beta1": bf(0.1 * np.random.standard_normal(D) * s)}


def reference(x, W_qkv, b_qkv, g1, beta1):
    h = layer_norm(f64(x), f64(g1), f64(beta1))
    qkv = (mxq(h, 2, "e4m3") @ mxq(f64(W_qkv), 1, "e4m3").T) + f64(b_qkv)
    qkv = qkv.reshape(B, T, 3, NH, HD)
    return qkv[:, :, 0].copy(), qkv[:, :, 1].copy(), qkv[:, :, 2].copy()

@@ -1,0 +1,249 @@
+from contextlib import ExitStack
+
+import concourse.mybir as mybir
+from concourse.masks import make_identity
+
+F32 = mybir.dt.float32
+BF16 = mybir.dt.bfloat16
+U32 = mybir.dt.uint32
+U8 = mybir.dt.uint8
+FP8X4 = mybir.dt.float8_e4m3fn_x4
+ACT = mybir.ActivationFunctionType
+ALU = mybir.AluOpType
+
+P = 128
+TOKENS = 512
+D = 1024
+FEATURES = 3 * D
+LN_EPS = 1e-6
+
+PACK = 4
+K_PASS = P * PACK
+PASSES = D // K_PASS
+PAIR = 2
+PAIRS = PACK // PAIR
+
+TOKEN_TILES = TOKENS // P
+TOKEN_GROUP = 2 * P
+TOKEN_GROUPS = TOKENS // TOKEN_GROUP
+
+CHUNK = 512
+CHUNKS = FEATURES // CHUNK
+ROW_TILES = CHUNK // P
+AHEAD = 2
+
+BN_WIDTH = 512
+BN_OUT = 6
+
+FLOPS = 2 * TOKENS * D * FEATURES
+
+
+def tile_block_pa_kernel(tc, x, W_qkv, b_qkv, g1, beta1, out_0, out_1, out_2):
+    nc = tc.nc
+    x_rows = x.flatten_outer_dims()
+    out_rows = [o.rearrange("b t h d -> (b t) (h d)") for o in (out_0, out_1, out_2)]
+
+    with ExitStack() as ctx:
+        keep = ctx.enter_context(tc.tile_pool(name="keep", bufs=1))
+        small = ctx.enter_context(tc.tile_pool(name="small", bufs=TOKEN_TILES))
+        normed = ctx.enter_context(tc.tile_pool(name="normed", bufs=TOKEN_TILES))
+        grouped = ctx.enter_context(tc.tile_pool(name="grouped", bufs=4))
+        results = ctx.enter_context(tc.tile_pool(name="results", bufs=8))
+        flip_banks = ctx.enter_context(tc.psum_pool(name="flip_banks", bufs=4))
+        sum_banks = ctx.enter_context(tc.psum_pool(name="sum_banks", bufs=4))
+
+        x_sb = keep.tile([P, TOKEN_TILES, D], BF16)
+        for i in range(TOKEN_TILES):
+            nc.sync.dma_start(out=x_sb[:, i, :], in_=x_rows[i * P : (i + 1) * P, :])
+        w_sb = keep.tile([P, CHUNKS, ROW_TILES, D], BF16)
+        for c in range(CHUNKS):
+            nc.sync.dma_start(
+                out=w_sb[:, c, :, :],
+                in_=W_qkv[c * CHUNK : (c + 1) * CHUNK, :].rearrange("(r p) k -> p r k", p=P),
+            )
+        w_words = w_sb[:].bitcast(F32)
+
+        gain_rows = keep.tile([P, K_PASS], BF16)
+        nc.vector.memset(gain_rows[:], 0.0)
+        nc.scalar.dma_start(
+            out=gain_rows[0:PASSES, :], in_=g1.rearrange("(r c) -> r c", c=K_PASS)
+        )
+        nc.scalar.dma_start(
+            out=gain_rows[PASSES : 2 * PASSES, :],
+            in_=beta1.rearrange("(r c) -> r c", c=K_PASS),
+        )
+        bias_rows = keep.tile([P, CHUNK], BF16)
+        nc.vector.memset(bias_rows[:], 0.0)
+        nc.scalar.dma_start(
+            out=bias_rows[0:CHUNKS, :], in_=b_qkv.rearrange("(r c) -> r c", c=CHUNK)
+        )
+
+        eps_col = keep.tile([P, 1], F32)
+        nc.vector.memset(eps_col[:], LN_EPS)
+        table_warmer = keep.tile([P, 1], F32)
+        nc.scalar.activation(out=table_warmer[:], in_=eps_col[:], func=ACT.Sqrt)
+        ident_f32 = keep.tile([P, P], F32)
+        make_identity(nc, ident_f32[:])
+        ident_bf16 = keep.tile([P, P], BF16)
+        make_identity(nc, ident_bf16[:])
+
+        gain_flipped = flip_banks.tile([P, PAIRS, P], F32, tag="flip")
+        gain_words = gain_rows[:].bitcast(F32)
+        for u in range(PAIRS):
+            nc.tensor.transpose(gain_flipped[:, u, :], gain_words[:, u::PAIRS], ident_f32[:])
+        gain_pairs = keep.tile([P, 2 * PASSES * PAIRS], F32)
+        nc.vector.tensor_copy(
+            out=gain_pairs[:].rearrange("p (r u) -> p r u", u=PAIRS),
+            in_=gain_flipped[:, :, 0 : 2 * PASSES].rearrange("p u r -> p r u"),
+        )
+        gain_cols = keep.tile([P, 2 * PASSES * PACK], F32)
+        nc.vector.tensor_copy(out=gain_cols[:], in_=gain_pairs[:].bitcast(BF16))
+        beta_at = PASSES * PACK
+
+        bias_all = keep.tile([P, FEATURES], BF16)
+        for b in range(CHUNKS // 2):
+            bias_bank = flip_banks.tile([P, 2 * CHUNK], BF16, tag="flip")
+            for half in range(2):
+                c = 2 * b + half
+                nc.tensor.matmul(
+                    out=bias_bank[:, half * CHUNK : (half + 1) * CHUNK],
+                    lhsT=ident_bf16[:, c : c + 1].to_broadcast([P, P]),
+                    rhs=bias_rows[:],
+                    start=True,
+                    stop=True,
+                )
+            nc.scalar.copy(out=bias_all[:, 2 * b * CHUNK : 2 * (b + 1) * CHUNK], in_=bias_bank[:])
+
+        h_codes = keep.tile([P, PASSES, TOKENS], U32, align_bytes=64)
+        h_scales = keep.tile([P, PASSES, TOKENS], U8, align_bytes=64)
+        w_codes = keep.tile([P, CHUNKS, PASSES, CHUNK], U32, align_bytes=64)
+        w_scales = keep.tile([P, CHUNKS, PASSES, CHUNK], U8, align_bytes=64)
+        h_planes = keep.tile([P, PASSES, PACK, TOKENS], BF16)
+        h_grouped = keep.tile([P, PASSES, TOKENS, PACK], BF16, align_bytes=64)
+
+        def normalise(i):
+            stats = small.tile([P, D // BN_WIDTH, BN_OUT], F32)
+            for s in range(D // BN_WIDTH):
+                nc.vector.bn_stats(
+                    out=stats[:, s, :], in_=x_sb[:, i, s * BN_WIDTH : (s + 1) * BN_WIDTH]
+                )
+            mean_var = small.tile([P, 2], F32)
+            nc.vector.bn_aggr(out=mean_var[:], in_=stats[:].rearrange("p s d -> p (s d)"))
+            std = small.tile([P, 1], F32)
+            nc.scalar.activation(out=std[:], in_=mean_var[:, 1:2], func=ACT.Sqrt, bias=eps_col[:])
+            rstd = small.tile([P, 1], F32)
+            nc.vector.reciprocal(out=rstd[:], in_=std[:])
+            neg_mean = small.tile([P, 1], F32)
+            nc.vector.tensor_scalar_mul(out=neg_mean[:], in0=mean_var[:, 0:1], scalar1=-1.0)
+            xn = normed.tile([P, PACK, D // PACK], F32)
+            nc.gpsimd.tensor_scalar(
+                out=xn[:],
+                in0=x_sb[:, i, :].rearrange("p (j t) -> p t j", t=PACK),
+                scalar1=neg_mean[:],
+                scalar2=rstd[:],
+                op0=ALU.add,
+                op1=ALU.mult,
+            )
+            return xn
+
+        def quantise_h(group, xn_tiles):
+            tokens = slice(group * TOKEN_GROUP, (group + 1) * TOKEN_GROUP)
+            for b in range(PASSES * PAIRS):
+                g, u = divmod(b, PAIRS)
+                flipped = sum_banks.tile([P, PAIR, TOKEN_GROUP], F32, tag="sum")
+                for r, xn in enumerate(xn_tiles):
+                    for e in range(PAIR):
+                        nc.tensor.transpose(
+                            flipped[:, e, r * P : (r + 1) * P],
+                            xn[:, PAIR * u + e, g * P : (g + 1) * P],
+                            ident_f32[:],
+                        )
+                for e in range(PAIR):
+                    col = PAIR * b + e
+                    if b % 2 == 0:
+                        nc.scalar.activation(
+                            out=h_planes[:, g, PAIR * u + e, tokens],
+                            in_=flipped[:, e, :],
+                            func=ACT.Identity,
+                            scale=gain_cols[:, col : col + 1],
+                            bias=gain_cols[:, beta_at + col : beta_at + col + 1],
+                        )
+                    else:
+                        nc.vector.tensor_scalar(
+                            out=h_planes[:, g, PAIR * u + e, tokens],
+                            in0=flipped[:, e, :],
+                            scalar1=gain_cols[:, col : col + 1],
+                            scalar2=gain_cols[:, beta_at + col : beta_at + col + 1],
+                            op0=ALU.mult,
+                            op1=ALU.add,
+                        )
+            for g in range(PASSES):
+                nc.vector.tensor_copy(
+                    out=h_grouped[:, g, tokens, :],
+                    in_=h_planes[:, g, :, tokens].rearrange("p t n -> p n t"),
+                )
+            for g in range(PASSES):
+                nc.vector.quantize_mx(
+                    out=h_codes[:, g, tokens].bitcast(FP8X4),
+                    scales=h_scales[:, g, tokens],
+                    in_=h_grouped[:, g, tokens, :].rearrange("p n t -> p (n t)"),
+                )
+
+        def prepare_weights(c):
+            for g in range(PASSES):
+                w_grouped = grouped.tile([P, CHUNK * PACK], BF16, align_bytes=64)
+                w_grouped_words = w_grouped[:].bitcast(F32).rearrange(
+                    "p (r f u) -> p r f u", r=ROW_TILES, u=2
+                )
+                for half in range(2):
+                    flipped = flip_banks.tile([P, 2, 2, P], F32, tag="flip")
+                    for r in range(2):
+                        for u in range(PAIRS):
+                            nc.tensor.transpose(
+                                flipped[:, r, u, :],
+                                w_words[
+                                    :, c, 2 * half + r, g * PAIRS * P + u : (g + 1) * PAIRS * P : PAIRS
+                                ],
+                                ident_f32[:],
+                            )
+                    nc.scalar.copy(
+                        out=w_grouped_words[:, 2 * half : 2 * half + 2, :, :],
+                        in_=flipped[:].rearrange("p r u f -> p r f u"),
+                    )
+                nc.vector.quantize_mx(
+                    out=w_codes[:, c, g, :].bitcast(FP8X4),
+                    scales=w_scales[:, c, g, :],
+                    in_=w_grouped[:],
+                )
+
+        def multiply(c):
+            columns = slice((c % 2) * CHUNK, (c % 2 + 1) * CHUNK)
+            for i in range(TOKEN_TILES):
+                rows = slice(i * P, (i + 1) * P)
+                sums = sum_banks.tile([P, CHUNK], F32, tag="sum")
+                for g in range(PASSES):
+                    nc.tensor.matmul_mx(
+                        out=sums[:],
+                        lhsT=h_codes[:, g, rows].bitcast(FP8X4),
+                        lhsT_scale=h_scales[:, g, rows],
+                        rhs=w_codes[:, c, g, :].bitcast(FP8X4),
+                        rhs_scale=w_scales[:, c, g, :],
+                        start=(g == 0),
+                        stop=(g == PASSES - 1),
+                    )
+                result = results.tile([P, CHUNK], F32)
+                nc.vector.tensor_tensor(
+                    out=result[:],
+                    in0=sums[:],
+                    in1=bias_all[:, c * CHUNK : (c + 1) * CHUNK],
+                    op=ALU.add,
+                )
+                nc.sync.dma_start(out=out_rows[c // 2][rows, columns], in_=result[:])
+
+        for group in range(TOKEN_GROUPS):
+            quantise_h(group, [normalise(2 * group), normalise(2 * group + 1)])
+            prepare_weights(group)
+        for c in range(CHUNKS):
+            if c + AHEAD < CHUNKS:
+                prepare_weights(c + AHEAD)
+            multiply(c)

@@ -24,12 +24,13 @@ PAIR = 2
 PAIRS = PACK // PAIR
 
 TOKEN_TILES = TOKENS // P
-TOKEN_GROUP = 2 * P
-TOKEN_GROUPS = TOKENS // TOKEN_GROUP
+GROUP_TILES = 2
+TOKEN_GROUP = GROUP_TILES * P
 
 CHUNK = 512
 CHUNKS = FEATURES // CHUNK
 ROW_TILES = CHUNK // P
+HALF_TILES = ROW_TILES // 2
 AHEAD = 2
 
 BN_WIDTH = 512
@@ -47,36 +48,34 @@ def tile_block_pa_kernel(tc, x, W_qkv, b_qkv, g1, beta1, out_0, out_1, out_2):
         keep = ctx.enter_context(tc.tile_pool(name="keep", bufs=1))
         small = ctx.enter_context(tc.tile_pool(name="small", bufs=TOKEN_TILES))
         normed = ctx.enter_context(tc.tile_pool(name="normed", bufs=TOKEN_TILES))
-        grouped = ctx.enter_context(tc.tile_pool(name="grouped", bufs=4))
+        grouped = ctx.enter_context(tc.tile_pool(name="grouped", bufs=CHUNKS))
         results = ctx.enter_context(tc.tile_pool(name="results", bufs=8))
+        plains = ctx.enter_context(tc.tile_pool(name="plains", bufs=3))
         flip_banks = ctx.enter_context(tc.psum_pool(name="flip_banks", bufs=4))
         sum_banks = ctx.enter_context(tc.psum_pool(name="sum_banks", bufs=4))
+        ctx.enter_context(tc.manual_schedule())
+
+        vectors = keep.tile([P, CHUNK], BF16)
+        nc.vector.memset(vectors[:].bitcast(U32), 0)
+        for row, vector in ((0, g1), (PASSES, beta1)):
+            nc.scalar.dma_start(
+                out=vectors[row : row + PASSES, :], in_=vector.rearrange("(r c) -> r c", c=CHUNK)
+            )
 
         x_sb = keep.tile([P, TOKEN_TILES, D], BF16)
+        w_sb = keep.tile([P, FEATURES // P, D], BF16)
         for i in range(TOKEN_TILES):
-            nc.sync.dma_start(out=x_sb[:, i, :], in_=x_rows[i * P : (i + 1) * P, :])
-        w_sb = keep.tile([P, CHUNKS, ROW_TILES, D], BF16)
-        for c in range(CHUNKS):
+            rows = slice(i * P, (i + 1) * P)
+            nc.sync.dma_start(out=x_sb[:, i, :], in_=x_rows[rows, :])
+            nc.sync.dma_start(out=w_sb[:, i, :], in_=W_qkv[rows, :])
+        for r in range(TOKEN_TILES, FEATURES // P, HALF_TILES):
             nc.sync.dma_start(
-                out=w_sb[:, c, :, :],
-                in_=W_qkv[c * CHUNK : (c + 1) * CHUNK, :].rearrange("(r p) k -> p r k", p=P),
+                out=w_sb[:, r : r + HALF_TILES, :],
+                in_=W_qkv[r * P : (r + HALF_TILES) * P, :].rearrange("(r p) k -> p r k", p=P),
             )
+        bias_all = keep.tile([P, FEATURES], BF16)
+        nc.sync.dma_start(out=bias_all[:], in_=b_qkv.partition_broadcast(P))
         w_words = w_sb[:].bitcast(F32)
-
-        gain_rows = keep.tile([P, K_PASS], BF16)
-        nc.vector.memset(gain_rows[:], 0.0)
-        nc.scalar.dma_start(
-            out=gain_rows[0:PASSES, :], in_=g1.rearrange("(r c) -> r c", c=K_PASS)
-        )
-        nc.scalar.dma_start(
-            out=gain_rows[PASSES : 2 * PASSES, :],
-            in_=beta1.rearrange("(r c) -> r c", c=K_PASS),
-        )
-        bias_rows = keep.tile([P, CHUNK], BF16)
-        nc.vector.memset(bias_rows[:], 0.0)
-        nc.scalar.dma_start(
-            out=bias_rows[0:CHUNKS, :], in_=b_qkv.rearrange("(r c) -> r c", c=CHUNK)
-        )
 
         eps_col = keep.tile([P, 1], F32)
         nc.vector.memset(eps_col[:], LN_EPS)
@@ -87,41 +86,31 @@ def tile_block_pa_kernel(tc, x, W_qkv, b_qkv, g1, beta1, out_0, out_1, out_2):
         ident_bf16 = keep.tile([P, P], BF16)
         make_identity(nc, ident_bf16[:])
 
-        gain_flipped = flip_banks.tile([P, PAIRS, P], F32, tag="flip")
-        gain_words = gain_rows[:].bitcast(F32)
-        for u in range(PAIRS):
-            nc.tensor.transpose(gain_flipped[:, u, :], gain_words[:, u::PAIRS], ident_f32[:])
-        gain_pairs = keep.tile([P, 2 * PASSES * PAIRS], F32)
-        nc.vector.tensor_copy(
-            out=gain_pairs[:].rearrange("p (r u) -> p r u", u=PAIRS),
-            in_=gain_flipped[:, :, 0 : 2 * PASSES].rearrange("p u r -> p r u"),
-        )
-        gain_cols = keep.tile([P, 2 * PASSES * PACK], F32)
-        nc.vector.tensor_copy(out=gain_cols[:], in_=gain_pairs[:].bitcast(BF16))
-        beta_at = PASSES * PACK
-
-        bias_all = keep.tile([P, FEATURES], BF16)
-        for b in range(CHUNKS // 2):
-            bias_bank = flip_banks.tile([P, 2 * CHUNK], BF16, tag="flip")
-            for half in range(2):
-                c = 2 * b + half
-                nc.tensor.matmul(
-                    out=bias_bank[:, half * CHUNK : (half + 1) * CHUNK],
-                    lhsT=ident_bf16[:, c : c + 1].to_broadcast([P, P]),
-                    rhs=bias_rows[:],
-                    start=True,
-                    stop=True,
-                )
-            nc.scalar.copy(out=bias_all[:, 2 * b * CHUNK : 2 * (b + 1) * CHUNK], in_=bias_bank[:])
-
         h_codes = keep.tile([P, PASSES, TOKENS], U32, align_bytes=64)
         h_scales = keep.tile([P, PASSES, TOKENS], U8, align_bytes=64)
         w_codes = keep.tile([P, CHUNKS, PASSES, CHUNK], U32, align_bytes=64)
         w_scales = keep.tile([P, CHUNKS, PASSES, CHUNK], U8, align_bytes=64)
         h_planes = keep.tile([P, PASSES, PACK, TOKENS], BF16)
         h_grouped = keep.tile([P, PASSES, TOKENS, PACK], BF16, align_bytes=64)
+        gain_cols = keep.tile([P, 2 * PASSES * PACK], F32)
+        beta_at = PASSES * PACK
 
-        def normalise(i):
+        def spread_gains():
+            gain_flipped = flip_banks.tile([P, PAIRS, P], F32, tag="flip")
+            for u in range(PAIRS):
+                nc.tensor.transpose(
+                    gain_flipped[:, u, :], vectors[:].bitcast(F32)[:, u::PAIRS], ident_f32[:]
+                )
+            gain_pairs = keep.tile([P, 2 * PASSES * PAIRS], F32)
+            nc.vector.tensor_copy(
+                out=gain_pairs[:].rearrange("p (r u) -> p r u", u=PAIRS),
+                in_=gain_flipped[:, :, 0 : 2 * PASSES].rearrange("p u r -> p r u"),
+            )
+            nc.vector.tensor_copy(out=gain_cols[:], in_=gain_pairs[:].bitcast(BF16))
+
+        mean_vars, stds, xns = [], [], []
+
+        def measure(i):
             stats = small.tile([P, D // BN_WIDTH, BN_OUT], F32)
             for s in range(D // BN_WIDTH):
                 nc.vector.bn_stats(
@@ -131,52 +120,73 @@ def tile_block_pa_kernel(tc, x, W_qkv, b_qkv, g1, beta1, out_0, out_1, out_2):
             nc.vector.bn_aggr(out=mean_var[:], in_=stats[:].rearrange("p s d -> p (s d)"))
             std = small.tile([P, 1], F32)
             nc.scalar.activation(out=std[:], in_=mean_var[:, 1:2], func=ACT.Sqrt, bias=eps_col[:])
-            rstd = small.tile([P, 1], F32)
-            nc.vector.reciprocal(out=rstd[:], in_=std[:])
-            neg_mean = small.tile([P, 1], F32)
-            nc.vector.tensor_scalar_mul(out=neg_mean[:], in0=mean_var[:, 0:1], scalar1=-1.0)
-            xn = normed.tile([P, PACK, D // PACK], F32)
-            nc.gpsimd.tensor_scalar(
-                out=xn[:],
-                in0=x_sb[:, i, :].rearrange("p (j t) -> p t j", t=PACK),
-                scalar1=neg_mean[:],
-                scalar2=rstd[:],
-                op0=ALU.add,
-                op1=ALU.mult,
-            )
-            return xn
+            mean_vars.append(mean_var)
+            stds.append(std)
 
-        def quantise_h(group, xn_tiles):
+        def normalise(i, engine):
+            rstd = small.tile([P, 1], F32)
+            nc.vector.reciprocal(out=rstd[:], in_=stds[i][:])
+            xn = normed.tile([P, PACK, D // PACK], F32)
+            planes = x_sb[:, i, :].rearrange("p (j t) -> p t j", t=PACK)
+            mean = mean_vars[i][:, 0:1]
+            if engine is nc.scalar:
+                shift = small.tile([P, 1], F32)
+                nc.vector.scalar_tensor_tensor(
+                    out=shift[:], in0=mean, scalar=-1.0, in1=rstd[:], op0=ALU.mult, op1=ALU.mult
+                )
+                nc.scalar.activation(
+                    out=xn[:], in_=planes, func=ACT.Identity, scale=rstd[:], bias=shift[:]
+                )
+            else:
+                neg_mean = small.tile([P, 1], F32)
+                nc.vector.tensor_scalar_mul(out=neg_mean[:], in0=mean, scalar1=-1.0)
+                engine.tensor_scalar(
+                    out=xn[:],
+                    in0=planes,
+                    scalar1=neg_mean[:],
+                    scalar2=rstd[:],
+                    op0=ALU.add,
+                    op1=ALU.mult,
+                )
+            xns.append(xn)
+
+        def flip_h(group, vector_banks=()):
             tokens = slice(group * TOKEN_GROUP, (group + 1) * TOKEN_GROUP)
+            banks = []
             for b in range(PASSES * PAIRS):
                 g, u = divmod(b, PAIRS)
                 flipped = sum_banks.tile([P, PAIR, TOKEN_GROUP], F32, tag="sum")
-                for r, xn in enumerate(xn_tiles):
+                for r in range(GROUP_TILES):
                     for e in range(PAIR):
                         nc.tensor.transpose(
                             flipped[:, e, r * P : (r + 1) * P],
-                            xn[:, PAIR * u + e, g * P : (g + 1) * P],
+                            xns[group * GROUP_TILES + r][:, PAIR * u + e, g * P : (g + 1) * P],
                             ident_f32[:],
                         )
+                banks.append(flipped)
+            for b, flipped in enumerate(banks):
+                g, u = divmod(b, PAIRS)
                 for e in range(PAIR):
                     col = PAIR * b + e
-                    if b % 2 == 0:
+                    gain = gain_cols[:, col : col + 1]
+                    beta = gain_cols[:, beta_at + col : beta_at + col + 1]
+                    plane = h_planes[:, g, PAIR * u + e, tokens]
+                    if b not in vector_banks:
                         nc.scalar.activation(
-                            out=h_planes[:, g, PAIR * u + e, tokens],
-                            in_=flipped[:, e, :],
-                            func=ACT.Identity,
-                            scale=gain_cols[:, col : col + 1],
-                            bias=gain_cols[:, beta_at + col : beta_at + col + 1],
+                            out=plane, in_=flipped[:, e, :], func=ACT.Identity, scale=gain, bias=beta
                         )
                     else:
                         nc.vector.tensor_scalar(
-                            out=h_planes[:, g, PAIR * u + e, tokens],
+                            out=plane,
                             in0=flipped[:, e, :],
-                            scalar1=gain_cols[:, col : col + 1],
-                            scalar2=gain_cols[:, beta_at + col : beta_at + col + 1],
+                            scalar1=gain,
+                            scalar2=beta,
                             op0=ALU.mult,
                             op1=ALU.add,
                         )
+
+        def quantise_h(group):
+            tokens = slice(group * TOKEN_GROUP, (group + 1) * TOKEN_GROUP)
             for g in range(PASSES):
                 nc.vector.tensor_copy(
                     out=h_grouped[:, g, tokens, :],
@@ -189,61 +199,87 @@ def tile_block_pa_kernel(tc, x, W_qkv, b_qkv, g1, beta1, out_0, out_1, out_2):
                     in_=h_grouped[:, g, tokens, :].rearrange("p n t -> p (n t)"),
                 )
 
-        def prepare_weights(c):
-            for g in range(PASSES):
-                w_grouped = grouped.tile([P, CHUNK * PACK], BF16, align_bytes=64)
-                w_grouped_words = w_grouped[:].bitcast(F32).rearrange(
-                    "p (r f u) -> p r f u", r=ROW_TILES, u=2
+        w_grouped = [None] * CHUNKS
+
+        def flip_weights(c, *row_tiles, copy=nc.scalar.copy):
+            if w_grouped[c] is None:
+                w_grouped[c] = grouped.tile(
+                    [P, PASSES, CHUNK * PACK], BF16, align_bytes=64, name="w_grouped"
                 )
-                for half in range(2):
-                    flipped = flip_banks.tile([P, 2, 2, P], F32, tag="flip")
-                    for r in range(2):
-                        for u in range(PAIRS):
-                            nc.tensor.transpose(
-                                flipped[:, r, u, :],
-                                w_words[
-                                    :, c, 2 * half + r, g * PAIRS * P + u : (g + 1) * PAIRS * P : PAIRS
-                                ],
-                                ident_f32[:],
-                            )
-                    nc.scalar.copy(
-                        out=w_grouped_words[:, 2 * half : 2 * half + 2, :, :],
-                        in_=flipped[:].rearrange("p r u f -> p r f u"),
-                    )
+            words = w_grouped[c][:].bitcast(F32).rearrange("p g (f u) -> p g f u", u=PAIRS)
+            for r in row_tiles:
+                flipped = flip_banks.tile([P, PASSES, PAIRS, P], F32, tag="flip")
+                for g in range(PASSES):
+                    for u in range(PAIRS):
+                        nc.tensor.transpose(
+                            flipped[:, g, u, :],
+                            w_words[
+                                :, c * ROW_TILES + r, g * PAIRS * P + u : (g + 1) * PAIRS * P : PAIRS
+                            ],
+                            ident_f32[:],
+                        )
+                copy(
+                    out=words[:, :, r * P : (r + 1) * P, :],
+                    in_=flipped[:].rearrange("p g u f -> p g f u"),
+                )
+
+        def quantise_weights(c):
+            for g in range(PASSES):
                 nc.vector.quantize_mx(
                     out=w_codes[:, c, g, :].bitcast(FP8X4),
                     scales=w_scales[:, c, g, :],
-                    in_=w_grouped[:],
+                    in_=w_grouped[c][:, g, :],
                 )
 
-        def multiply(c):
+        def multiply(c, i, share=False):
             columns = slice((c % 2) * CHUNK, (c % 2 + 1) * CHUNK)
-            for i in range(TOKEN_TILES):
-                rows = slice(i * P, (i + 1) * P)
-                sums = sum_banks.tile([P, CHUNK], F32, tag="sum")
-                for g in range(PASSES):
-                    nc.tensor.matmul_mx(
-                        out=sums[:],
-                        lhsT=h_codes[:, g, rows].bitcast(FP8X4),
-                        lhsT_scale=h_scales[:, g, rows],
-                        rhs=w_codes[:, c, g, :].bitcast(FP8X4),
-                        rhs_scale=w_scales[:, c, g, :],
-                        start=(g == 0),
-                        stop=(g == PASSES - 1),
-                    )
-                result = results.tile([P, CHUNK], F32)
-                nc.vector.tensor_tensor(
-                    out=result[:],
-                    in0=sums[:],
-                    in1=bias_all[:, c * CHUNK : (c + 1) * CHUNK],
-                    op=ALU.add,
+            rows = slice(i * P, (i + 1) * P)
+            sums = sum_banks.tile([P, CHUNK], F32, tag="sum")
+            for g in range(PASSES):
+                nc.tensor.matmul_mx(
+                    out=sums[:],
+                    lhsT=h_codes[:, g, rows].bitcast(FP8X4),
+                    lhsT_scale=h_scales[:, g, rows],
+                    rhs=w_codes[:, c, g, :].bitcast(FP8X4),
+                    rhs_scale=w_scales[:, c, g, :],
+                    start=(g == 0),
+                    stop=(g == PASSES - 1),
                 )
-                nc.sync.dma_start(out=out_rows[c // 2][rows, columns], in_=result[:])
+            result = results.tile([P, CHUNK], F32)
+            bias = bias_all[:, c * CHUNK : (c + 1) * CHUNK]
+            if share:
+                plain = plains.tile([P, CHUNK], F32)
+                nc.scalar.copy(out=plain[:], in_=sums[:])
+                nc.gpsimd.tensor_tensor(out=result[:], in0=plain[:], in1=bias, op=ALU.add)
+            else:
+                nc.vector.tensor_tensor(out=result[:], in0=sums[:], in1=bias, op=ALU.add)
+            nc.sync.dma_start(out=out_rows[c // 2][rows, columns], in_=result[:])
 
-        for group in range(TOKEN_GROUPS):
-            quantise_h(group, [normalise(2 * group), normalise(2 * group + 1)])
-            prepare_weights(group)
+        measure(0)
+        flip_weights(0, 0)
+        measure(1)
+        normalise(0, nc.gpsimd)
+        flip_weights(0, 1)
+        measure(2)
+        normalise(1, nc.gpsimd)
+        flip_weights(0, 2, 3)
+        measure(3)
+        normalise(2, nc.gpsimd)
+        spread_gains()
+        normalise(3, nc.gpsimd)
+        flip_weights(1, 0)
+        flip_h(0, (1, 3))
+        flip_weights(1, 1, 2, 3)
+        quantise_h(0)
+        quantise_weights(0)
+        flip_h(1, (1, 3))
+        flip_weights(2, 0, 1, 2, 3)
+        quantise_h(1)
         for c in range(CHUNKS):
-            if c + AHEAD < CHUNKS:
-                prepare_weights(c + AHEAD)
-            multiply(c)
+            if c < 2:
+                quantise_weights(c + 1)
+            for i in range(TOKEN_TILES):
+                multiply(c, i, i == (0 if c == CHUNKS - 1 else 2))
+            if c + 3 < CHUNKS:
+                flip_weights(c + 3, 0, 1, 2, 3)
+                quantise_weights(c + 3)

@@ -108,6 +108,12 @@ def tile_block_pa_kernel(tc, x, W_qkv, b_qkv, g1, beta1, out_0, out_1, out_2):
             )
             nc.vector.tensor_copy(out=gain_cols[:], in_=gain_pairs[:].bitcast(BF16))
 
+        def keep_warm(bank, times):
+            for step in range(times):
+                nc.tensor.matmul(
+                    out=bank, lhsT=ident_f32[:], rhs=ident_f32[:], start=True, stop=True
+                )
+
         mean_vars, stds, xns = [], [], []
 
         def measure(i):
@@ -156,6 +162,7 @@ def tile_block_pa_kernel(tc, x, W_qkv, b_qkv, g1, beta1, out_0, out_1, out_2):
             for b in range(PASSES * PAIRS):
                 g, u = divmod(b, PAIRS)
                 flipped = sum_banks.tile([P, PAIR, TOKEN_GROUP], F32, tag="sum")
+                keep_warm(flipped[:, 0, 0:P], 1 if u == 0 else 0)
                 for r in range(GROUP_TILES):
                     for e in range(PAIR):
                         nc.tensor.transpose(
@@ -201,7 +208,7 @@ def tile_block_pa_kernel(tc, x, W_qkv, b_qkv, g1, beta1, out_0, out_1, out_2):
 
         w_grouped = [None] * CHUNKS
 
-        def flip_weights(c, *row_tiles, copy=nc.scalar.copy):
+        def flip_weights(c, *row_tiles, copy=nc.scalar.copy, warm=0):
             if w_grouped[c] is None:
                 w_grouped[c] = grouped.tile(
                     [P, PASSES, CHUNK * PACK], BF16, align_bytes=64, name="w_grouped"
@@ -209,6 +216,7 @@ def tile_block_pa_kernel(tc, x, W_qkv, b_qkv, g1, beta1, out_0, out_1, out_2):
             words = w_grouped[c][:].bitcast(F32).rearrange("p g (f u) -> p g f u", u=PAIRS)
             for r in row_tiles:
                 flipped = flip_banks.tile([P, PASSES, PAIRS, P], F32, tag="flip")
+                keep_warm(flipped[:, 0, 0, :], warm)
                 for g in range(PASSES):
                     for u in range(PAIRS):
                         nc.tensor.transpose(
@@ -256,30 +264,31 @@ def tile_block_pa_kernel(tc, x, W_qkv, b_qkv, g1, beta1, out_0, out_1, out_2):
             nc.sync.dma_start(out=out_rows[c // 2][rows, columns], in_=result[:])
 
         measure(0)
-        flip_weights(0, 0)
+        flip_weights(0, 0, warm=5)
         measure(1)
         normalise(0, nc.gpsimd)
-        flip_weights(0, 1)
+        flip_weights(0, 1, warm=2)
         measure(2)
         normalise(1, nc.gpsimd)
-        flip_weights(0, 2, 3)
+        flip_weights(0, 2, 3, warm=2)
         measure(3)
         normalise(2, nc.gpsimd)
         spread_gains()
         normalise(3, nc.gpsimd)
-        flip_weights(1, 0)
+        flip_weights(1, 0, warm=1)
         flip_h(0, (1, 3))
-        flip_weights(1, 1, 2, 3)
+        flip_weights(1, 1, 2, 3, warm=1)
         quantise_h(0)
         quantise_weights(0)
         flip_h(1, (1, 3))
-        flip_weights(2, 0, 1, 2, 3)
+        flip_weights(2, 0, 1, 2, 3, warm=1)
         quantise_h(1)
         for c in range(CHUNKS):
             if c < 2:
                 quantise_weights(c + 1)
             for i in range(TOKEN_TILES):
                 multiply(c, i, i == (0 if c == CHUNKS - 1 else 2))
+                if c + 3 < CHUNKS and i % 2 == 1:
+                    flip_weights(c + 3, i - 1, i)
             if c + 3 < CHUNKS:
-                flip_weights(c + 3, 0, 1, 2, 3)
                 quantise_weights(c + 3)

@@ -24,14 +24,14 @@ PAIR = 2
 PAIRS = PACK // PAIR
 
 TOKEN_TILES = TOKENS // P
-GROUP_TILES = 2
-TOKEN_GROUP = GROUP_TILES * P
 
 CHUNK = 512
 CHUNKS = FEATURES // CHUNK
 ROW_TILES = CHUNK // P
 HALF_TILES = ROW_TILES // 2
 AHEAD = 2
+
+BIAS_AFTER = {2 * ROW_TILES: slice(0, 2 * CHUNK), FEATURES // P: slice(2 * CHUNK, FEATURES)}
 
 BN_WIDTH = 512
 BN_OUT = 6
@@ -51,6 +51,7 @@ def tile_block_pa_kernel(tc, x, W_qkv, b_qkv, g1, beta1, out_0, out_1, out_2):
         grouped = ctx.enter_context(tc.tile_pool(name="grouped", bufs=CHUNKS))
         results = ctx.enter_context(tc.tile_pool(name="results", bufs=8))
         plains = ctx.enter_context(tc.tile_pool(name="plains", bufs=3))
+        w_gathered = ctx.enter_context(tc.tile_pool(name="w_gathered", bufs=6))
         flip_banks = ctx.enter_context(tc.psum_pool(name="flip_banks", bufs=4))
         sum_banks = ctx.enter_context(tc.psum_pool(name="sum_banks", bufs=4))
         ctx.enter_context(tc.manual_schedule())
@@ -68,13 +69,17 @@ def tile_block_pa_kernel(tc, x, W_qkv, b_qkv, g1, beta1, out_0, out_1, out_2):
             rows = slice(i * P, (i + 1) * P)
             nc.sync.dma_start(out=x_sb[:, i, :], in_=x_rows[rows, :])
             nc.sync.dma_start(out=w_sb[:, i, :], in_=W_qkv[rows, :])
+        bias_all = keep.tile([P, FEATURES], BF16)
         for r in range(TOKEN_TILES, FEATURES // P, HALF_TILES):
             nc.sync.dma_start(
                 out=w_sb[:, r : r + HALF_TILES, :],
                 in_=W_qkv[r * P : (r + HALF_TILES) * P, :].rearrange("(r p) k -> p r k", p=P),
             )
-        bias_all = keep.tile([P, FEATURES], BF16)
-        nc.sync.dma_start(out=bias_all[:], in_=b_qkv.partition_broadcast(P))
+            if r + HALF_TILES in BIAS_AFTER:
+                columns = BIAS_AFTER[r + HALF_TILES]
+                nc.sync.dma_start(
+                    out=bias_all[:, columns], in_=b_qkv[columns].partition_broadcast(P)
+                )
         w_words = w_sb[:].bitcast(F32)
 
         eps_col = keep.tile([P, 1], F32)
@@ -86,12 +91,12 @@ def tile_block_pa_kernel(tc, x, W_qkv, b_qkv, g1, beta1, out_0, out_1, out_2):
         ident_bf16 = keep.tile([P, P], BF16)
         make_identity(nc, ident_bf16[:])
 
-        h_codes = keep.tile([P, PASSES, TOKENS], U32, align_bytes=64)
-        h_scales = keep.tile([P, PASSES, TOKENS], U8, align_bytes=64)
+        h_codes = keep.tile([P, TOKEN_TILES, PASSES, P], U32, align_bytes=64)
+        h_scales = keep.tile([P, TOKEN_TILES, PASSES, P], U8, align_bytes=64)
         w_codes = keep.tile([P, CHUNKS, PASSES, CHUNK], U32, align_bytes=64)
         w_scales = keep.tile([P, CHUNKS, PASSES, CHUNK], U8, align_bytes=64)
-        h_planes = keep.tile([P, PASSES, PACK, TOKENS], BF16)
-        h_grouped = keep.tile([P, PASSES, TOKENS, PACK], BF16, align_bytes=64)
+        h_planes = keep.tile([P, TOKEN_TILES, PASSES, PACK, P], BF16)
+        h_grouped = keep.tile([P, TOKEN_TILES, PASSES, P, PACK], BF16, align_bytes=64)
         gain_cols = keep.tile([P, 2 * PASSES * PACK], F32)
         beta_at = PASSES * PACK
 
@@ -156,57 +161,70 @@ def tile_block_pa_kernel(tc, x, W_qkv, b_qkv, g1, beta1, out_0, out_1, out_2):
                 )
             xns.append(xn)
 
-        def flip_h(group, vector_banks=()):
-            tokens = slice(group * TOKEN_GROUP, (group + 1) * TOKEN_GROUP)
-            banks = []
-            for b in range(PASSES * PAIRS):
-                g, u = divmod(b, PAIRS)
-                flipped = sum_banks.tile([P, PAIR, TOKEN_GROUP], F32, tag="sum")
-                keep_warm(flipped[:, 0, 0:P], 1 if u == 0 else 0)
-                for r in range(GROUP_TILES):
-                    for e in range(PAIR):
-                        nc.tensor.transpose(
-                            flipped[:, e, r * P : (r + 1) * P],
-                            xns[group * GROUP_TILES + r][:, PAIR * u + e, g * P : (g + 1) * P],
-                            ident_f32[:],
-                        )
-                banks.append(flipped)
-            for b, flipped in enumerate(banks):
-                g, u = divmod(b, PAIRS)
-                for e in range(PAIR):
-                    col = PAIR * b + e
+        def flip_h(i, engines, warm=0):
+            for g, engine in enumerate(engines):
+                flipped = sum_banks.tile([P, PACK, P], F32, tag="sum")
+                keep_warm(flipped[:, 0, :], warm)
+                for t in range(PACK):
+                    nc.tensor.transpose(
+                        flipped[:, t, :], xns[i][:, t, g * P : (g + 1) * P], ident_f32[:]
+                    )
+                for t in range(PACK):
+                    col = PACK * g + t
                     gain = gain_cols[:, col : col + 1]
                     beta = gain_cols[:, beta_at + col : beta_at + col + 1]
-                    plane = h_planes[:, g, PAIR * u + e, tokens]
-                    if b not in vector_banks:
+                    if engine is nc.scalar:
                         nc.scalar.activation(
-                            out=plane, in_=flipped[:, e, :], func=ACT.Identity, scale=gain, bias=beta
+                            out=h_planes[:, i, g, t, :],
+                            in_=flipped[:, t, :],
+                            func=ACT.Identity,
+                            scale=gain,
+                            bias=beta,
                         )
                     else:
                         nc.vector.tensor_scalar(
-                            out=plane,
-                            in0=flipped[:, e, :],
+                            out=h_planes[:, i, g, t, :],
+                            in0=flipped[:, t, :],
                             scalar1=gain,
                             scalar2=beta,
                             op0=ALU.mult,
                             op1=ALU.add,
                         )
 
-        def quantise_h(group):
-            tokens = slice(group * TOKEN_GROUP, (group + 1) * TOKEN_GROUP)
-            for g in range(PASSES):
-                nc.vector.tensor_copy(
-                    out=h_grouped[:, g, tokens, :],
-                    in_=h_planes[:, g, :, tokens].rearrange("p t n -> p n t"),
+        def regroup_h(i, engine=nc.vector):
+            planes = h_planes[:, i, :, :, :].rearrange("p g t n -> p g n t")
+            if engine is nc.gpsimd:
+                engine.tensor_scalar(
+                    out=h_grouped[:, i, :, :, :],
+                    in0=planes,
+                    scalar1=1.0,
+                    scalar2=0.0,
+                    op0=ALU.mult,
+                    op1=ALU.add,
                 )
-            for g in range(PASSES):
-                nc.vector.quantize_mx(
-                    out=h_codes[:, g, tokens].bitcast(FP8X4),
-                    scales=h_scales[:, g, tokens],
-                    in_=h_grouped[:, g, tokens, :].rearrange("p n t -> p (n t)"),
-                )
+            else:
+                engine.tensor_copy(out=h_grouped[:, i, :, :, :], in_=planes)
+
+        def quantise_h(i):
+            nc.vector.quantize_mx(
+                out=h_codes[:, i, :, :].rearrange("p g n -> p (g n)").bitcast(FP8X4),
+                scales=h_scales[:, i, :, :].rearrange("p g n -> p (g n)"),
+                in_=h_grouped[:, i, :, :, :].rearrange("p g n t -> p (g n t)"),
+            )
 
         w_grouped = [None] * CHUNKS
+
+        gathered_tiles = {}
+
+        def gather_pairs(c, r, copy):
+            gathered = w_gathered.tile([P, PASSES, PAIRS, P], F32, name="gathered")
+            copy(
+                out=gathered[:].rearrange("p g u j -> p g j u"),
+                in_=w_words[:, c * ROW_TILES + r, :].rearrange(
+                    "p (g j u) -> p g j u", g=PASSES, u=PAIRS
+                ),
+            )
+            gathered_tiles[c, r] = gathered
 
         def flip_weights(c, *row_tiles, copy=nc.scalar.copy, warm=0):
             if w_grouped[c] is None:
@@ -219,20 +237,20 @@ def tile_block_pa_kernel(tc, x, W_qkv, b_qkv, g1, beta1, out_0, out_1, out_2):
                 keep_warm(flipped[:, 0, 0, :], warm)
                 for g in range(PASSES):
                     for u in range(PAIRS):
-                        nc.tensor.transpose(
-                            flipped[:, g, u, :],
-                            w_words[
+                        if (c, r) in gathered_tiles:
+                            pairs = gathered_tiles[c, r][:, g, u, :]
+                        else:
+                            pairs = w_words[
                                 :, c * ROW_TILES + r, g * PAIRS * P + u : (g + 1) * PAIRS * P : PAIRS
-                            ],
-                            ident_f32[:],
-                        )
+                            ]
+                        nc.tensor.transpose(flipped[:, g, u, :], pairs, ident_f32[:])
                 copy(
                     out=words[:, :, r * P : (r + 1) * P, :],
                     in_=flipped[:].rearrange("p g u f -> p g f u"),
                 )
 
-        def quantise_weights(c):
-            for g in range(PASSES):
+        def quantise_weights(c, passes=range(PASSES)):
+            for g in passes:
                 nc.vector.quantize_mx(
                     out=w_codes[:, c, g, :].bitcast(FP8X4),
                     scales=w_scales[:, c, g, :],
@@ -246,8 +264,8 @@ def tile_block_pa_kernel(tc, x, W_qkv, b_qkv, g1, beta1, out_0, out_1, out_2):
             for g in range(PASSES):
                 nc.tensor.matmul_mx(
                     out=sums[:],
-                    lhsT=h_codes[:, g, rows].bitcast(FP8X4),
-                    lhsT_scale=h_scales[:, g, rows],
+                    lhsT=h_codes[:, i, g, :].bitcast(FP8X4),
+                    lhsT_scale=h_scales[:, i, g, :],
                     rhs=w_codes[:, c, g, :].bitcast(FP8X4),
                     rhs_scale=w_scales[:, c, g, :],
                     start=(g == 0),
@@ -263,32 +281,84 @@ def tile_block_pa_kernel(tc, x, W_qkv, b_qkv, g1, beta1, out_0, out_1, out_2):
                 nc.vector.tensor_tensor(out=result[:], in0=sums[:], in1=bias, op=ALU.add)
             nc.sync.dma_start(out=out_rows[c // 2][rows, columns], in_=result[:])
 
+        S, V, G = nc.scalar, nc.vector, nc.gpsimd
         measure(0)
         flip_weights(0, 0, warm=5)
         measure(1)
-        normalise(0, nc.gpsimd)
+        normalise(0, G)
         flip_weights(0, 1, warm=2)
         measure(2)
-        normalise(1, nc.gpsimd)
-        flip_weights(0, 2, 3, warm=2)
-        measure(3)
-        normalise(2, nc.gpsimd)
+        normalise(1, G)
+        flip_weights(0, 2, warm=1)
         spread_gains()
-        normalise(3, nc.gpsimd)
-        flip_weights(1, 0, warm=1)
-        flip_h(0, (1, 3))
-        flip_weights(1, 1, 2, 3, warm=1)
+        measure(3)
+        flip_weights(0, 3, warm=1)
+        normalise(2, G)
+        flip_h(0, (S, V))
+        normalise(3, G)
+        flip_weights(1, 0, 1, warm=1)
+        quantise_weights(0, (0,))
+        regroup_h(0)
+        quantise_weights(0, (1,))
+        flip_h(1, (S, V))
         quantise_h(0)
-        quantise_weights(0)
-        flip_h(1, (1, 3))
-        flip_weights(2, 0, 1, 2, 3, warm=1)
+        flip_weights(1, 2, warm=1)
+        regroup_h(1)
+        flip_h(2, (S, S), warm=1)
         quantise_h(1)
-        for c in range(CHUNKS):
-            if c < 2:
-                quantise_weights(c + 1)
-            for i in range(TOKEN_TILES):
-                multiply(c, i, i == (0 if c == CHUNKS - 1 else 2))
-                if c + 3 < CHUNKS and i % 2 == 1:
-                    flip_weights(c + 3, i - 1, i)
-            if c + 3 < CHUNKS:
-                quantise_weights(c + 3)
+        multiply(0, 0)
+        flip_weights(1, 3)
+        regroup_h(2, G)
+        flip_h(3, (S, V))
+        flip_weights(2, 0)
+        multiply(0, 1)
+        quantise_weights(1)
+        regroup_h(3, G)
+        quantise_h(2)
+        flip_weights(2, 1)
+        multiply(1, 0)
+        multiply(1, 1)
+        quantise_h(3)
+        gather_pairs(3, 0, nc.scalar.copy)
+        gather_pairs(3, 1, nc.vector.tensor_copy)
+        flip_weights(2, 2, 3)
+        multiply(0, 2, False)
+        multiply(1, 2, False)
+        gather_pairs(3, 2, nc.scalar.copy)
+        gather_pairs(3, 3, nc.vector.tensor_copy)
+        flip_weights(3, 0, 1)
+        quantise_weights(2)
+        multiply(0, 3, False)
+        multiply(1, 3, False)
+        gather_pairs(4, 0, nc.scalar.copy)
+        gather_pairs(4, 1, nc.vector.tensor_copy)
+        flip_weights(3, 2, 3)
+        multiply(2, 0, False)
+        multiply(2, 1, False)
+        gather_pairs(4, 2, nc.scalar.copy)
+        gather_pairs(4, 3, nc.vector.tensor_copy)
+        flip_weights(4, 0, 1)
+        quantise_weights(3)
+        multiply(2, 2, False)
+        multiply(2, 3, False)
+        gather_pairs(5, 0, nc.scalar.copy)
+        gather_pairs(5, 1, nc.vector.tensor_copy)
+        flip_weights(4, 2, 3)
+        multiply(3, 0, False)
+        multiply(3, 1, False)
+        gather_pairs(5, 2, nc.scalar.copy)
+        gather_pairs(5, 3, nc.vector.tensor_copy)
+        flip_weights(5, 0, 1)
+        quantise_weights(4)
+        multiply(3, 2, False)
+        multiply(3, 3, False)
+        flip_weights(5, 2, 3)
+        multiply(4, 0, False)
+        multiply(4, 1, False)
+        quantise_weights(5)
+        multiply(4, 2, False)
+        multiply(4, 3, False)
+        multiply(5, 0, False)
+        multiply(5, 1, False)
+        multiply(5, 2, False)
+        multiply(5, 3, False)

@@ -49,9 +49,9 @@ def tile_block_pa_kernel(tc, x, W_qkv, b_qkv, g1, beta1, out_0, out_1, out_2):
         small = ctx.enter_context(tc.tile_pool(name="small", bufs=TOKEN_TILES))
         normed = ctx.enter_context(tc.tile_pool(name="normed", bufs=TOKEN_TILES))
         grouped = ctx.enter_context(tc.tile_pool(name="grouped", bufs=CHUNKS))
-        results = ctx.enter_context(tc.tile_pool(name="results", bufs=8))
+        results = ctx.enter_context(tc.tile_pool(name="results", bufs=12))
         plains = ctx.enter_context(tc.tile_pool(name="plains", bufs=3))
-        w_gathered = ctx.enter_context(tc.tile_pool(name="w_gathered", bufs=6))
+        w_gathered = ctx.enter_context(tc.tile_pool(name="w_gathered", bufs=8))
         flip_banks = ctx.enter_context(tc.psum_pool(name="flip_banks", bufs=4))
         sum_banks = ctx.enter_context(tc.psum_pool(name="sum_banks", bufs=4))
         ctx.enter_context(tc.manual_schedule())
@@ -85,7 +85,7 @@ def tile_block_pa_kernel(tc, x, W_qkv, b_qkv, g1, beta1, out_0, out_1, out_2):
         eps_col = keep.tile([P, 1], F32)
         nc.vector.memset(eps_col[:], LN_EPS)
         table_warmer = keep.tile([P, 1], F32)
-        nc.scalar.activation(out=table_warmer[:], in_=eps_col[:], func=ACT.Sqrt)
+        nc.scalar.activation(out=table_warmer[:], in_=eps_col[:], func=ACT.Abs_reciprocal_sqrt)
         ident_f32 = keep.tile([P, P], F32)
         make_identity(nc, ident_f32[:])
         ident_bf16 = keep.tile([P, P], BF16)
@@ -119,7 +119,7 @@ def tile_block_pa_kernel(tc, x, W_qkv, b_qkv, g1, beta1, out_0, out_1, out_2):
                     out=bank, lhsT=ident_f32[:], rhs=ident_f32[:], start=True, stop=True
                 )
 
-        mean_vars, stds, xns = [], [], []
+        mean_vars, rstds, xns = [], [], []
 
         def measure(i):
             stats = small.tile([P, D // BN_WIDTH, BN_OUT], F32)
@@ -129,14 +129,20 @@ def tile_block_pa_kernel(tc, x, W_qkv, b_qkv, g1, beta1, out_0, out_1, out_2):
                 )
             mean_var = small.tile([P, 2], F32)
             nc.vector.bn_aggr(out=mean_var[:], in_=stats[:].rearrange("p s d -> p (s d)"))
-            std = small.tile([P, 1], F32)
-            nc.scalar.activation(out=std[:], in_=mean_var[:, 1:2], func=ACT.Sqrt, bias=eps_col[:])
             mean_vars.append(mean_var)
-            stds.append(std)
+
+        def invert_std(i):
+            rstd = small.tile([P, 1], F32)
+            nc.scalar.activation(
+                out=rstd[:],
+                in_=mean_vars[i][:, 1:2],
+                func=ACT.Abs_reciprocal_sqrt,
+                bias=eps_col[:],
+            )
+            rstds.append(rstd)
 
         def normalise(i, engine):
-            rstd = small.tile([P, 1], F32)
-            nc.vector.reciprocal(out=rstd[:], in_=stds[i][:])
+            rstd = rstds[i]
             xn = normed.tile([P, PACK, D // PACK], F32)
             planes = x_sb[:, i, :].rearrange("p (j t) -> p t j", t=PACK)
             mean = mean_vars[i][:, 0:1]
@@ -150,7 +156,9 @@ def tile_block_pa_kernel(tc, x, W_qkv, b_qkv, g1, beta1, out_0, out_1, out_2):
                 )
             else:
                 neg_mean = small.tile([P, 1], F32)
-                nc.vector.tensor_scalar_mul(out=neg_mean[:], in0=mean, scalar1=-1.0)
+                engine.tensor_scalar(
+                    out=neg_mean[:], in0=mean, scalar1=-1.0, scalar2=0.0, op0=ALU.mult, op1=ALU.add
+                )
                 engine.tensor_scalar(
                     out=xn[:],
                     in0=planes,
@@ -161,35 +169,40 @@ def tile_block_pa_kernel(tc, x, W_qkv, b_qkv, g1, beta1, out_0, out_1, out_2):
                 )
             xns.append(xn)
 
-        def flip_h(i, engines, warm=0):
-            for g, engine in enumerate(engines):
-                flipped = sum_banks.tile([P, PACK, P], F32, tag="sum")
+        h_banks = {}
+
+        def flip_h(i, warm=0):
+            for g in range(PASSES):
+                flipped = sum_banks.tile([P, PACK, P], F32, tag="sum", name="h_flipped")
                 keep_warm(flipped[:, 0, :], warm)
                 for t in range(PACK):
                     nc.tensor.transpose(
                         flipped[:, t, :], xns[i][:, t, g * P : (g + 1) * P], ident_f32[:]
                     )
-                for t in range(PACK):
-                    col = PACK * g + t
-                    gain = gain_cols[:, col : col + 1]
-                    beta = gain_cols[:, beta_at + col : beta_at + col + 1]
-                    if engine is nc.scalar:
-                        nc.scalar.activation(
-                            out=h_planes[:, i, g, t, :],
-                            in_=flipped[:, t, :],
-                            func=ACT.Identity,
-                            scale=gain,
-                            bias=beta,
-                        )
-                    else:
-                        nc.vector.tensor_scalar(
-                            out=h_planes[:, i, g, t, :],
-                            in0=flipped[:, t, :],
-                            scalar1=gain,
-                            scalar2=beta,
-                            op0=ALU.mult,
-                            op1=ALU.add,
-                        )
+                h_banks[i, g] = flipped
+
+        def scale_h(i, g, engine):
+            for t in range(PACK):
+                col = PACK * g + t
+                gain = gain_cols[:, col : col + 1]
+                beta = gain_cols[:, beta_at + col : beta_at + col + 1]
+                if engine is nc.scalar:
+                    nc.scalar.activation(
+                        out=h_planes[:, i, g, t, :],
+                        in_=h_banks[i, g][:, t, :],
+                        func=ACT.Identity,
+                        scale=gain,
+                        bias=beta,
+                    )
+                else:
+                    nc.vector.tensor_scalar(
+                        out=h_planes[:, i, g, t, :],
+                        in0=h_banks[i, g][:, t, :],
+                        scalar1=gain,
+                        scalar2=beta,
+                        op0=ALU.mult,
+                        op1=ALU.add,
+                    )
 
         def regroup_h(i, engine=nc.vector):
             planes = h_planes[:, i, :, :, :].rearrange("p g t n -> p g n t")
@@ -202,6 +215,8 @@ def tile_block_pa_kernel(tc, x, W_qkv, b_qkv, g1, beta1, out_0, out_1, out_2):
                     op0=ALU.mult,
                     op1=ALU.add,
                 )
+            elif engine is nc.scalar:
+                engine.copy(out=h_grouped[:, i, :, :, :], in_=planes)
             else:
                 engine.tensor_copy(out=h_grouped[:, i, :, :, :], in_=planes)
 
@@ -226,28 +241,32 @@ def tile_block_pa_kernel(tc, x, W_qkv, b_qkv, g1, beta1, out_0, out_1, out_2):
             )
             gathered_tiles[c, r] = gathered
 
-        def flip_weights(c, *row_tiles, copy=nc.scalar.copy, warm=0):
+        w_banks = {}
+
+        def flip_weights(c, r, warm=0):
+            flipped = flip_banks.tile([P, PASSES, PAIRS, P], F32, tag="flip", name="w_flipped")
+            keep_warm(flipped[:, 0, 0, :], warm)
+            for g in range(PASSES):
+                for u in range(PAIRS):
+                    if (c, r) in gathered_tiles:
+                        pairs = gathered_tiles[c, r][:, g, u, :]
+                    else:
+                        pairs = w_words[
+                            :, c * ROW_TILES + r, g * PAIRS * P + u : (g + 1) * PAIRS * P : PAIRS
+                        ]
+                    nc.tensor.transpose(flipped[:, g, u, :], pairs, ident_f32[:])
+            w_banks[c, r] = flipped
+
+        def group_weights(c, r, copy):
             if w_grouped[c] is None:
                 w_grouped[c] = grouped.tile(
                     [P, PASSES, CHUNK * PACK], BF16, align_bytes=64, name="w_grouped"
                 )
             words = w_grouped[c][:].bitcast(F32).rearrange("p g (f u) -> p g f u", u=PAIRS)
-            for r in row_tiles:
-                flipped = flip_banks.tile([P, PASSES, PAIRS, P], F32, tag="flip")
-                keep_warm(flipped[:, 0, 0, :], warm)
-                for g in range(PASSES):
-                    for u in range(PAIRS):
-                        if (c, r) in gathered_tiles:
-                            pairs = gathered_tiles[c, r][:, g, u, :]
-                        else:
-                            pairs = w_words[
-                                :, c * ROW_TILES + r, g * PAIRS * P + u : (g + 1) * PAIRS * P : PAIRS
-                            ]
-                        nc.tensor.transpose(flipped[:, g, u, :], pairs, ident_f32[:])
-                copy(
-                    out=words[:, :, r * P : (r + 1) * P, :],
-                    in_=flipped[:].rearrange("p g u f -> p g f u"),
-                )
+            copy(
+                out=words[:, :, r * P : (r + 1) * P, :],
+                in_=w_banks[c, r][:].rearrange("p g u f -> p g f u"),
+            )
 
         def quantise_weights(c, passes=range(PASSES)):
             for g in passes:
@@ -257,10 +276,10 @@ def tile_block_pa_kernel(tc, x, W_qkv, b_qkv, g1, beta1, out_0, out_1, out_2):
                     in_=w_grouped[c][:, g, :],
                 )
 
-        def multiply(c, i, share=False):
-            columns = slice((c % 2) * CHUNK, (c % 2 + 1) * CHUNK)
-            rows = slice(i * P, (i + 1) * P)
-            sums = sum_banks.tile([P, CHUNK], F32, tag="sum")
+        sums_banks = {}
+
+        def multiply(c, i):
+            sums = sum_banks.tile([P, CHUNK], F32, tag="sum", name="sums")
             for g in range(PASSES):
                 nc.tensor.matmul_mx(
                     out=sums[:],
@@ -271,6 +290,12 @@ def tile_block_pa_kernel(tc, x, W_qkv, b_qkv, g1, beta1, out_0, out_1, out_2):
                     start=(g == 0),
                     stop=(g == PASSES - 1),
                 )
+            sums_banks[c, i] = sums
+
+        def finish(c, i, share=False):
+            sums = sums_banks[c, i]
+            columns = slice((c % 2) * CHUNK, (c % 2 + 1) * CHUNK)
+            rows = slice(i * P, (i + 1) * P)
             result = results.tile([P, CHUNK], F32)
             bias = bias_all[:, c * CHUNK : (c + 1) * CHUNK]
             if share:
@@ -282,83 +307,155 @@ def tile_block_pa_kernel(tc, x, W_qkv, b_qkv, g1, beta1, out_0, out_1, out_2):
             nc.sync.dma_start(out=out_rows[c // 2][rows, columns], in_=result[:])
 
         S, V, G = nc.scalar, nc.vector, nc.gpsimd
+        SC, VC = nc.scalar.copy, nc.vector.tensor_copy
         measure(0)
+        invert_std(0)
         flip_weights(0, 0, warm=5)
         measure(1)
         normalise(0, G)
+        group_weights(0, 0, SC)
         flip_weights(0, 1, warm=2)
         measure(2)
-        normalise(1, G)
-        flip_weights(0, 2, warm=1)
+        invert_std(1)
         spread_gains()
+        normalise(1, G)
+        group_weights(0, 1, SC)
+        flip_weights(0, 2, warm=1)
         measure(3)
-        flip_weights(0, 3, warm=1)
+        invert_std(2)
+        flip_h(0)
+        group_weights(0, 2, VC)
         normalise(2, G)
-        flip_h(0, (S, V))
-        normalise(3, G)
-        flip_weights(1, 0, 1, warm=1)
+        scale_h(0, 0, S)
+        flip_weights(0, 3)
+        scale_h(0, 1, S)
+        flip_weights(1, 0)
+        invert_std(3)
+        flip_h(1)
+        normalise(3, V)
+        scale_h(1, 0, S)
+        flip_weights(1, 1)
+        group_weights(0, 3, VC)
+        scale_h(1, 1, S)
+        flip_h(2)
+        regroup_h(0, V)
+        group_weights(1, 0, SC)
+        flip_weights(1, 2)
         quantise_weights(0, (0,))
-        regroup_h(0)
+        scale_h(2, 0, S)
+        flip_h(3)
         quantise_weights(0, (1,))
-        flip_h(1, (S, V))
-        quantise_h(0)
-        flip_weights(1, 2, warm=1)
-        regroup_h(1)
-        flip_h(2, (S, S), warm=1)
-        quantise_h(1)
-        multiply(0, 0)
+        scale_h(2, 1, S)
         flip_weights(1, 3)
-        regroup_h(2, G)
-        flip_h(3, (S, V))
-        flip_weights(2, 0)
+        quantise_h(0)
+        scale_h(3, 0, S)
+        multiply(0, 0)
+        regroup_h(1, V)
+        scale_h(3, 1, S)
+        group_weights(1, 1, VC)
+        group_weights(1, 2, SC)
+        quantise_h(1)
+        group_weights(1, 3, SC)
         multiply(0, 1)
-        quantise_weights(1)
-        regroup_h(3, G)
-        quantise_h(2)
+        regroup_h(2, V)
+        flip_weights(2, 0)
+        regroup_h(3, V)
+        group_weights(2, 0, SC)
         flip_weights(2, 1)
-        multiply(1, 0)
-        multiply(1, 1)
+        quantise_h(2)
+        group_weights(2, 1, SC)
+        multiply(0, 2)
         quantise_h(3)
-        gather_pairs(3, 0, nc.scalar.copy)
-        gather_pairs(3, 1, nc.vector.tensor_copy)
-        flip_weights(2, 2, 3)
-        multiply(0, 2, False)
-        multiply(1, 2, False)
-        gather_pairs(3, 2, nc.scalar.copy)
-        gather_pairs(3, 3, nc.vector.tensor_copy)
-        flip_weights(3, 0, 1)
-        quantise_weights(2)
-        multiply(0, 3, False)
-        multiply(1, 3, False)
-        gather_pairs(4, 0, nc.scalar.copy)
-        gather_pairs(4, 1, nc.vector.tensor_copy)
-        flip_weights(3, 2, 3)
-        multiply(2, 0, False)
-        multiply(2, 1, False)
-        gather_pairs(4, 2, nc.scalar.copy)
-        gather_pairs(4, 3, nc.vector.tensor_copy)
-        flip_weights(4, 0, 1)
-        quantise_weights(3)
-        multiply(2, 2, False)
-        multiply(2, 3, False)
-        gather_pairs(5, 0, nc.scalar.copy)
-        gather_pairs(5, 1, nc.vector.tensor_copy)
-        flip_weights(4, 2, 3)
-        multiply(3, 0, False)
-        multiply(3, 1, False)
-        gather_pairs(5, 2, nc.scalar.copy)
-        gather_pairs(5, 3, nc.vector.tensor_copy)
-        flip_weights(5, 0, 1)
-        quantise_weights(4)
-        multiply(3, 2, False)
-        multiply(3, 3, False)
-        flip_weights(5, 2, 3)
-        multiply(4, 0, False)
-        multiply(4, 1, False)
-        quantise_weights(5)
-        multiply(4, 2, False)
-        multiply(4, 3, False)
-        multiply(5, 0, False)
-        multiply(5, 1, False)
-        multiply(5, 2, False)
-        multiply(5, 3, False)
+        gather_pairs(3, 0, SC)
+        multiply(0, 3)
+        finish(0, 0)
+        gather_pairs(3, 1, SC)
+        flip_weights(2, 2)
+        quantise_weights(1, (0,))
+        group_weights(2, 2, SC)
+        flip_weights(2, 3)
+        finish(0, 1)
+        group_weights(2, 3, SC)
+        quantise_weights(1, (1,))
+        gather_pairs(3, 2, SC)
+        multiply(1, 0)
+        finish(0, 2)
+        gather_pairs(3, 3, SC)
+        multiply(1, 1)
+        finish(0, 3)
+        flip_weights(3, 0)
+        finish(1, 0)
+        group_weights(3, 0, SC)
+        flip_weights(3, 1)
+        finish(1, 1)
+        group_weights(3, 1, SC)
+        multiply(1, 2)
+        quantise_weights(2, (0,))
+        gather_pairs(4, 0, SC)
+        multiply(1, 3)
+        quantise_weights(2, (1,))
+        gather_pairs(4, 1, SC)
+        flip_weights(3, 2)
+        finish(1, 2)
+        group_weights(3, 2, SC)
+        flip_weights(3, 3)
+        finish(1, 3)
+        group_weights(3, 3, SC)
+        multiply(2, 0)
+        finish(2, 0)
+        gather_pairs(4, 2, SC)
+        multiply(2, 1)
+        finish(2, 1)
+        gather_pairs(4, 3, SC)
+        flip_weights(4, 0)
+        quantise_weights(3, (0,))
+        group_weights(4, 0, SC)
+        flip_weights(4, 1)
+        quantise_weights(3, (1,))
+        group_weights(4, 1, SC)
+        multiply(2, 2)
+        finish(2, 2)
+        gather_pairs(5, 0, SC)
+        multiply(2, 3)
+        finish(2, 3)
+        flip_weights(4, 2)
+        group_weights(4, 2, SC)
+        flip_weights(4, 3)
+        group_weights(4, 3, SC)
+        multiply(3, 0)
+        finish(3, 0)
+        gather_pairs(5, 2, SC)
+        multiply(3, 1)
+        finish(3, 1)
+        flip_weights(5, 0)
+        quantise_weights(4, (0,))
+        group_weights(5, 0, SC)
+        flip_weights(5, 1)
+        quantise_weights(4, (1,))
+        group_weights(5, 1, SC)
+        multiply(3, 2)
+        finish(3, 2)
+        multiply(3, 3)
+        finish(3, 3)
+        flip_weights(5, 2)
+        group_weights(5, 2, SC)
+        flip_weights(5, 3)
+        group_weights(5, 3, SC)
+        multiply(4, 0)
+        finish(4, 0)
+        multiply(4, 1)
+        quantise_weights(5, (0,))
+        multiply(4, 2)
+        quantise_weights(5, (1,))
+        multiply(4, 3)
+        finish(4, 1)
+        multiply(5, 0)
+        finish(4, 2)
+        multiply(5, 1)
+        finish(4, 3)
+        multiply(5, 2)
+        finish(5, 0)
+        multiply(5, 3)
+        finish(5, 1)
+        finish(5, 2)
+        finish(5, 3)

@@ -33,6 +33,8 @@ AHEAD = 2
 
 BIAS_AFTER = {2 * ROW_TILES: slice(0, 2 * CHUNK), FEATURES // P: slice(2 * CHUNK, FEATURES)}
 
+RUN = 4
+
 BN_WIDTH = 512
 BN_OUT = 6
 
@@ -50,7 +52,6 @@ def tile_block_pa_kernel(tc, x, W_qkv, b_qkv, g1, beta1, out_0, out_1, out_2):
         normed = ctx.enter_context(tc.tile_pool(name="normed", bufs=TOKEN_TILES))
         grouped = ctx.enter_context(tc.tile_pool(name="grouped", bufs=CHUNKS))
         results = ctx.enter_context(tc.tile_pool(name="results", bufs=12))
-        plains = ctx.enter_context(tc.tile_pool(name="plains", bufs=3))
         w_gathered = ctx.enter_context(tc.tile_pool(name="w_gathered", bufs=8))
         flip_banks = ctx.enter_context(tc.psum_pool(name="flip_banks", bufs=4))
         sum_banks = ctx.enter_context(tc.psum_pool(name="sum_banks", bufs=4))
@@ -95,7 +96,7 @@ def tile_block_pa_kernel(tc, x, W_qkv, b_qkv, g1, beta1, out_0, out_1, out_2):
         h_scales = keep.tile([P, TOKEN_TILES, PASSES, P], U8, align_bytes=64)
         w_codes = keep.tile([P, CHUNKS, PASSES, CHUNK], U32, align_bytes=64)
         w_scales = keep.tile([P, CHUNKS, PASSES, CHUNK], U8, align_bytes=64)
-        h_planes = keep.tile([P, TOKEN_TILES, PASSES, PACK, P], BF16)
+        h_planes = keep.tile([P, TOKEN_TILES, PACK, PASSES, P], BF16)
         h_grouped = keep.tile([P, TOKEN_TILES, PASSES, P, PACK], BF16, align_bytes=64)
         gain_cols = keep.tile([P, 2 * PASSES * PACK], F32)
         beta_at = PASSES * PACK
@@ -188,7 +189,7 @@ def tile_block_pa_kernel(tc, x, W_qkv, b_qkv, g1, beta1, out_0, out_1, out_2):
                 beta = gain_cols[:, beta_at + col : beta_at + col + 1]
                 if engine is nc.scalar:
                     nc.scalar.activation(
-                        out=h_planes[:, i, g, t, :],
+                        out=h_planes[:, i, t, g, :],
                         in_=h_banks[i, g][:, t, :],
                         func=ACT.Identity,
                         scale=gain,
@@ -196,7 +197,7 @@ def tile_block_pa_kernel(tc, x, W_qkv, b_qkv, g1, beta1, out_0, out_1, out_2):
                     )
                 else:
                     nc.vector.tensor_scalar(
-                        out=h_planes[:, i, g, t, :],
+                        out=h_planes[:, i, t, g, :],
                         in0=h_banks[i, g][:, t, :],
                         scalar1=gain,
                         scalar2=beta,
@@ -204,21 +205,11 @@ def tile_block_pa_kernel(tc, x, W_qkv, b_qkv, g1, beta1, out_0, out_1, out_2):
                         op1=ALU.add,
                     )
 
-        def regroup_h(i, engine=nc.vector):
-            planes = h_planes[:, i, :, :, :].rearrange("p g t n -> p g n t")
-            if engine is nc.gpsimd:
-                engine.tensor_scalar(
-                    out=h_grouped[:, i, :, :, :],
-                    in0=planes,
-                    scalar1=1.0,
-                    scalar2=0.0,
-                    op0=ALU.mult,
-                    op1=ALU.add,
-                )
-            elif engine is nc.scalar:
-                engine.copy(out=h_grouped[:, i, :, :, :], in_=planes)
-            else:
-                engine.tensor_copy(out=h_grouped[:, i, :, :, :], in_=planes)
+        def regroup_h(i, engine):
+            engine.tensor_copy(
+                out=h_grouped[:, i, :, :, :].rearrange("p g (c n) t -> p (g c) t n", n=RUN),
+                in_=h_planes[:, i, :, :, :].rearrange("p t g (c n) -> p (g c) t n", n=RUN),
+            )
 
         def quantise_h(i):
             nc.vector.quantize_mx(
@@ -292,18 +283,16 @@ def tile_block_pa_kernel(tc, x, W_qkv, b_qkv, g1, beta1, out_0, out_1, out_2):
                 )
             sums_banks[c, i] = sums
 
-        def finish(c, i, share=False):
-            sums = sums_banks[c, i]
+        def finish(c, i):
             columns = slice((c % 2) * CHUNK, (c % 2 + 1) * CHUNK)
             rows = slice(i * P, (i + 1) * P)
             result = results.tile([P, CHUNK], F32)
-            bias = bias_all[:, c * CHUNK : (c + 1) * CHUNK]
-            if share:
-                plain = plains.tile([P, CHUNK], F32)
-                nc.scalar.copy(out=plain[:], in_=sums[:])
-                nc.gpsimd.tensor_tensor(out=result[:], in0=plain[:], in1=bias, op=ALU.add)
-            else:
-                nc.vector.tensor_tensor(out=result[:], in0=sums[:], in1=bias, op=ALU.add)
+            nc.vector.tensor_tensor(
+                out=result[:],
+                in0=sums_banks[c, i][:],
+                in1=bias_all[:, c * CHUNK : (c + 1) * CHUNK],
+                op=ALU.add,
+            )
             nc.sync.dma_start(out=out_rows[c // 2][rows, columns], in_=result[:])
 
         S, V, G = nc.scalar, nc.vector, nc.gpsimd

@@ -24,16 +24,16 @@ PAIR = 2
 PAIRS = PACK // PAIR
 
 TOKEN_TILES = TOKENS // P
-
 CHUNK = 512
 CHUNKS = FEATURES // CHUNK
 ROW_TILES = CHUNK // P
-HALF_TILES = ROW_TILES // 2
-AHEAD = 2
+W_TILES = CHUNKS * ROW_TILES
 
-BIAS_AFTER = {2 * ROW_TILES: slice(0, 2 * CHUNK), FEATURES // P: slice(2 * CHUNK, FEATURES)}
-
-RUN = 4
+EARLY = 2
+LOAD_TILES = 2
+STEP = 2
+GATHERED = 3
+GATHER_LEAD = ROW_TILES
 
 BN_WIDTH = 512
 BN_OUT = 6
@@ -51,76 +51,76 @@ def tile_block_pa_kernel(tc, x, W_qkv, b_qkv, g1, beta1, out_0, out_1, out_2):
         small = ctx.enter_context(tc.tile_pool(name="small", bufs=TOKEN_TILES))
         normed = ctx.enter_context(tc.tile_pool(name="normed", bufs=TOKEN_TILES))
         grouped = ctx.enter_context(tc.tile_pool(name="grouped", bufs=CHUNKS))
+        gathers = ctx.enter_context(tc.tile_pool(name="gathers", bufs=2 * GATHER_LEAD))
         results = ctx.enter_context(tc.tile_pool(name="results", bufs=12))
-        w_gathered = ctx.enter_context(tc.tile_pool(name="w_gathered", bufs=8))
         flip_banks = ctx.enter_context(tc.psum_pool(name="flip_banks", bufs=4))
         sum_banks = ctx.enter_context(tc.psum_pool(name="sum_banks", bufs=4))
         ctx.enter_context(tc.manual_schedule())
 
-        vectors = keep.tile([P, CHUNK], BF16)
+        vectors = keep.tile([P, K_PASS], BF16)
         nc.vector.memset(vectors[:].bitcast(U32), 0)
         for row, vector in ((0, g1), (PASSES, beta1)):
             nc.scalar.dma_start(
-                out=vectors[row : row + PASSES, :], in_=vector.rearrange("(r c) -> r c", c=CHUNK)
+                out=vectors[row : row + PASSES, :], in_=vector.rearrange("(r c) -> r c", c=K_PASS)
             )
 
         x_sb = keep.tile([P, TOKEN_TILES, D], BF16)
-        w_sb = keep.tile([P, FEATURES // P, D], BF16)
+        w_sb = keep.tile([P, W_TILES, D], BF16)
+        bias_all = keep.tile([P, FEATURES], BF16)
+
+        def load_weights(first, last):
+            for k in range(first, last, LOAD_TILES):
+                nc.sync.dma_start(
+                    out=w_sb[:, k : k + LOAD_TILES, :],
+                    in_=W_qkv[k * P : (k + LOAD_TILES) * P, :].rearrange("(r p) k -> p r k", p=P),
+                )
+
+        def load_bias(first, last):
+            nc.sync.dma_start(
+                out=bias_all[:, first:last], in_=b_qkv[first:last].partition_broadcast(P)
+            )
+
         for i in range(TOKEN_TILES):
             rows = slice(i * P, (i + 1) * P)
             nc.sync.dma_start(out=x_sb[:, i, :], in_=x_rows[rows, :])
             nc.sync.dma_start(out=w_sb[:, i, :], in_=W_qkv[rows, :])
-        bias_all = keep.tile([P, FEATURES], BF16)
-        for r in range(TOKEN_TILES, FEATURES // P, HALF_TILES):
-            nc.sync.dma_start(
-                out=w_sb[:, r : r + HALF_TILES, :],
-                in_=W_qkv[r * P : (r + HALF_TILES) * P, :].rearrange("(r p) k -> p r k", p=P),
-            )
-            if r + HALF_TILES in BIAS_AFTER:
-                columns = BIAS_AFTER[r + HALF_TILES]
-                nc.sync.dma_start(
-                    out=bias_all[:, columns], in_=b_qkv[columns].partition_broadcast(P)
-                )
+        load_weights(ROW_TILES, 3 * ROW_TILES)
+        load_bias(0, 2 * CHUNK)
+        load_weights(3 * ROW_TILES, W_TILES)
+        load_bias(2 * CHUNK, FEATURES)
         w_words = w_sb[:].bitcast(F32)
 
         eps_col = keep.tile([P, 1], F32)
         nc.vector.memset(eps_col[:], LN_EPS)
         table_warmer = keep.tile([P, 1], F32)
         nc.scalar.activation(out=table_warmer[:], in_=eps_col[:], func=ACT.Abs_reciprocal_sqrt)
-        ident_f32 = keep.tile([P, P], F32)
-        make_identity(nc, ident_f32[:])
-        ident_bf16 = keep.tile([P, P], BF16)
-        make_identity(nc, ident_bf16[:])
+        ident = keep.tile([P, P], F32)
+        make_identity(nc, ident[:])
 
         h_codes = keep.tile([P, TOKEN_TILES, PASSES, P], U32, align_bytes=64)
         h_scales = keep.tile([P, TOKEN_TILES, PASSES, P], U8, align_bytes=64)
         w_codes = keep.tile([P, CHUNKS, PASSES, CHUNK], U32, align_bytes=64)
         w_scales = keep.tile([P, CHUNKS, PASSES, CHUNK], U8, align_bytes=64)
-        h_planes = keep.tile([P, TOKEN_TILES, PACK, PASSES, P], BF16)
+        h_planes = keep.tile([P, TOKEN_TILES, PASSES, PACK, P], BF16)
         h_grouped = keep.tile([P, TOKEN_TILES, PASSES, P, PACK], BF16, align_bytes=64)
         gain_cols = keep.tile([P, 2 * PASSES * PACK], F32)
         beta_at = PASSES * PACK
 
+        mean_vars, rstds, xns, h_banks = {}, {}, {}, {}
+        gathered, w_banks, w_grouped, sums = {}, {}, {}, {}
+
         def spread_gains():
-            gain_flipped = flip_banks.tile([P, PAIRS, P], F32, tag="flip")
+            flipped = flip_banks.tile([P, PAIRS, P], F32, tag="flip", name="gain_flipped")
             for u in range(PAIRS):
                 nc.tensor.transpose(
-                    gain_flipped[:, u, :], vectors[:].bitcast(F32)[:, u::PAIRS], ident_f32[:]
+                    flipped[:, u, :], vectors[:].bitcast(F32)[:, u::PAIRS], ident[:]
                 )
-            gain_pairs = keep.tile([P, 2 * PASSES * PAIRS], F32)
+            pairs = keep.tile([P, 2 * PASSES * PAIRS], F32)
             nc.vector.tensor_copy(
-                out=gain_pairs[:].rearrange("p (r u) -> p r u", u=PAIRS),
-                in_=gain_flipped[:, :, 0 : 2 * PASSES].rearrange("p u r -> p r u"),
+                out=pairs[:].rearrange("p (r u) -> p r u", u=PAIRS),
+                in_=flipped[:, :, 0 : 2 * PASSES].rearrange("p u r -> p r u"),
             )
-            nc.vector.tensor_copy(out=gain_cols[:], in_=gain_pairs[:].bitcast(BF16))
-
-        def keep_warm(bank, times):
-            for step in range(times):
-                nc.tensor.matmul(
-                    out=bank, lhsT=ident_f32[:], rhs=ident_f32[:], start=True, stop=True
-                )
-
-        mean_vars, rstds, xns = [], [], []
+            nc.vector.tensor_copy(out=gain_cols[:], in_=pairs[:].bitcast(BF16))
 
         def measure(i):
             stats = small.tile([P, D // BN_WIDTH, BN_OUT], F32)
@@ -130,7 +130,7 @@ def tile_block_pa_kernel(tc, x, W_qkv, b_qkv, g1, beta1, out_0, out_1, out_2):
                 )
             mean_var = small.tile([P, 2], F32)
             nc.vector.bn_aggr(out=mean_var[:], in_=stats[:].rearrange("p s d -> p (s d)"))
-            mean_vars.append(mean_var)
+            mean_vars[i] = mean_var
 
         def invert_std(i):
             rstd = small.tile([P, 1], F32)
@@ -140,75 +140,54 @@ def tile_block_pa_kernel(tc, x, W_qkv, b_qkv, g1, beta1, out_0, out_1, out_2):
                 func=ACT.Abs_reciprocal_sqrt,
                 bias=eps_col[:],
             )
-            rstds.append(rstd)
+            rstds[i] = rstd
 
         def normalise(i, engine):
-            rstd = rstds[i]
+            neg_mean = small.tile([P, 1], F32)
+            engine.tensor_scalar(
+                out=neg_mean[:],
+                in0=mean_vars[i][:, 0:1],
+                scalar1=-1.0,
+                scalar2=0.0,
+                op0=ALU.mult,
+                op1=ALU.add,
+            )
             xn = normed.tile([P, PACK, D // PACK], F32)
-            planes = x_sb[:, i, :].rearrange("p (j t) -> p t j", t=PACK)
-            mean = mean_vars[i][:, 0:1]
-            if engine is nc.scalar:
-                shift = small.tile([P, 1], F32)
-                nc.vector.scalar_tensor_tensor(
-                    out=shift[:], in0=mean, scalar=-1.0, in1=rstd[:], op0=ALU.mult, op1=ALU.mult
-                )
-                nc.scalar.activation(
-                    out=xn[:], in_=planes, func=ACT.Identity, scale=rstd[:], bias=shift[:]
-                )
-            else:
-                neg_mean = small.tile([P, 1], F32)
-                engine.tensor_scalar(
-                    out=neg_mean[:], in0=mean, scalar1=-1.0, scalar2=0.0, op0=ALU.mult, op1=ALU.add
-                )
-                engine.tensor_scalar(
-                    out=xn[:],
-                    in0=planes,
-                    scalar1=neg_mean[:],
-                    scalar2=rstd[:],
-                    op0=ALU.add,
-                    op1=ALU.mult,
-                )
-            xns.append(xn)
+            engine.tensor_scalar(
+                out=xn[:],
+                in0=x_sb[:, i, :].rearrange("p (j t) -> p t j", t=PACK),
+                scalar1=neg_mean[:],
+                scalar2=rstds[i][:],
+                op0=ALU.add,
+                op1=ALU.mult,
+            )
+            xns[i] = xn
 
-        h_banks = {}
-
-        def flip_h(i, warm=0):
+        def flip_h(i):
             for g in range(PASSES):
                 flipped = sum_banks.tile([P, PACK, P], F32, tag="sum", name="h_flipped")
-                keep_warm(flipped[:, 0, :], warm)
                 for t in range(PACK):
                     nc.tensor.transpose(
-                        flipped[:, t, :], xns[i][:, t, g * P : (g + 1) * P], ident_f32[:]
+                        flipped[:, t, :], xns[i][:, t, g * P : (g + 1) * P], ident[:]
                     )
                 h_banks[i, g] = flipped
 
-        def scale_h(i, g, engine):
-            for t in range(PACK):
-                col = PACK * g + t
-                gain = gain_cols[:, col : col + 1]
-                beta = gain_cols[:, beta_at + col : beta_at + col + 1]
-                if engine is nc.scalar:
+        def scale_h(i):
+            for g in range(PASSES):
+                for t in range(PACK):
+                    col = PACK * g + t
                     nc.scalar.activation(
-                        out=h_planes[:, i, t, g, :],
+                        out=h_planes[:, i, g, t, :],
                         in_=h_banks[i, g][:, t, :],
                         func=ACT.Identity,
-                        scale=gain,
-                        bias=beta,
-                    )
-                else:
-                    nc.vector.tensor_scalar(
-                        out=h_planes[:, i, t, g, :],
-                        in0=h_banks[i, g][:, t, :],
-                        scalar1=gain,
-                        scalar2=beta,
-                        op0=ALU.mult,
-                        op1=ALU.add,
+                        scale=gain_cols[:, col : col + 1],
+                        bias=gain_cols[:, beta_at + col : beta_at + col + 1],
                     )
 
-        def regroup_h(i, engine):
-            engine.tensor_copy(
-                out=h_grouped[:, i, :, :, :].rearrange("p g (c n) t -> p (g c) t n", n=RUN),
-                in_=h_planes[:, i, :, :, :].rearrange("p t g (c n) -> p (g c) t n", n=RUN),
+        def regroup_h(i):
+            nc.vector.tensor_copy(
+                out=h_grouped[:, i, :, :, :],
+                in_=h_planes[:, i, :, :, :].rearrange("p g t n -> p g n t"),
             )
 
         def quantise_h(i):
@@ -218,62 +197,51 @@ def tile_block_pa_kernel(tc, x, W_qkv, b_qkv, g1, beta1, out_0, out_1, out_2):
                 in_=h_grouped[:, i, :, :, :].rearrange("p g n t -> p (g n t)"),
             )
 
-        w_grouped = [None] * CHUNKS
-
-        gathered_tiles = {}
-
-        def gather_pairs(c, r, copy):
-            gathered = w_gathered.tile([P, PASSES, PAIRS, P], F32, name="gathered")
-            copy(
-                out=gathered[:].rearrange("p g u j -> p g j u"),
-                in_=w_words[:, c * ROW_TILES + r, :].rearrange(
-                    "p (g j u) -> p g j u", g=PASSES, u=PAIRS
-                ),
+        def gather_words(k):
+            words = gathers.tile([P, PASSES, PAIRS, P], F32)
+            nc.scalar.copy(
+                out=words[:].rearrange("p g u j -> p g j u"),
+                in_=w_words[:, k, :].rearrange("p (g j u) -> p g j u", g=PASSES, u=PAIRS),
             )
-            gathered_tiles[c, r] = gathered
+            gathered[k] = words
 
-        w_banks = {}
-
-        def flip_weights(c, r, warm=0):
+        def flip_weights(k):
             flipped = flip_banks.tile([P, PASSES, PAIRS, P], F32, tag="flip", name="w_flipped")
-            keep_warm(flipped[:, 0, 0, :], warm)
             for g in range(PASSES):
                 for u in range(PAIRS):
-                    if (c, r) in gathered_tiles:
-                        pairs = gathered_tiles[c, r][:, g, u, :]
+                    if k in gathered:
+                        pairs = gathered[k][:, g, u, :]
                     else:
-                        pairs = w_words[
-                            :, c * ROW_TILES + r, g * PAIRS * P + u : (g + 1) * PAIRS * P : PAIRS
-                        ]
-                    nc.tensor.transpose(flipped[:, g, u, :], pairs, ident_f32[:])
-            w_banks[c, r] = flipped
+                        first = g * PAIRS * P + u
+                        pairs = w_words[:, k, first : (g + 1) * PAIRS * P : PAIRS]
+                    nc.tensor.transpose(flipped[:, g, u, :], pairs, ident[:])
+            w_banks[k] = flipped
 
-        def group_weights(c, r, copy):
-            if w_grouped[c] is None:
+        def group_weights(k, copy):
+            c, r = divmod(k, ROW_TILES)
+            if r == 0:
                 w_grouped[c] = grouped.tile(
                     [P, PASSES, CHUNK * PACK], BF16, align_bytes=64, name="w_grouped"
                 )
             words = w_grouped[c][:].bitcast(F32).rearrange("p g (f u) -> p g f u", u=PAIRS)
             copy(
                 out=words[:, :, r * P : (r + 1) * P, :],
-                in_=w_banks[c, r][:].rearrange("p g u f -> p g f u"),
+                in_=w_banks[k][:].rearrange("p g u f -> p g f u"),
             )
 
-        def quantise_weights(c, passes=range(PASSES)):
-            for g in passes:
+        def quantise_weights(c):
+            for g in range(PASSES):
                 nc.vector.quantize_mx(
                     out=w_codes[:, c, g, :].bitcast(FP8X4),
                     scales=w_scales[:, c, g, :],
                     in_=w_grouped[c][:, g, :],
                 )
 
-        sums_banks = {}
-
         def multiply(c, i):
-            sums = sum_banks.tile([P, CHUNK], F32, tag="sum", name="sums")
+            bank = sum_banks.tile([P, CHUNK], F32, tag="sum", name="sums")
             for g in range(PASSES):
                 nc.tensor.matmul_mx(
-                    out=sums[:],
+                    out=bank[:],
                     lhsT=h_codes[:, i, g, :].bitcast(FP8X4),
                     lhsT_scale=h_scales[:, i, g, :],
                     rhs=w_codes[:, c, g, :].bitcast(FP8X4),
@@ -281,170 +249,82 @@ def tile_block_pa_kernel(tc, x, W_qkv, b_qkv, g1, beta1, out_0, out_1, out_2):
                     start=(g == 0),
                     stop=(g == PASSES - 1),
                 )
-            sums_banks[c, i] = sums
+            sums[c, i] = bank
 
         def finish(c, i):
-            columns = slice((c % 2) * CHUNK, (c % 2 + 1) * CHUNK)
-            rows = slice(i * P, (i + 1) * P)
+            first = c * CHUNK
             result = results.tile([P, CHUNK], F32)
             nc.vector.tensor_tensor(
                 out=result[:],
-                in0=sums_banks[c, i][:],
-                in1=bias_all[:, c * CHUNK : (c + 1) * CHUNK],
+                in0=sums[c, i][:],
+                in1=bias_all[:, first : first + CHUNK],
                 op=ALU.add,
             )
-            nc.sync.dma_start(out=out_rows[c // 2][rows, columns], in_=result[:])
+            nc.sync.dma_start(
+                out=out_rows[first // D][i * P : (i + 1) * P, first % D : first % D + CHUNK],
+                in_=result[:],
+            )
 
-        S, V, G = nc.scalar, nc.vector, nc.gpsimd
-        SC, VC = nc.scalar.copy, nc.vector.tensor_copy
         measure(0)
+        flip_weights(0)
         invert_std(0)
-        flip_weights(0, 0, warm=5)
+        normalise(0, nc.gpsimd)
+        group_weights(0, nc.scalar.copy)
         measure(1)
-        normalise(0, G)
-        group_weights(0, 0, SC)
-        flip_weights(0, 1, warm=2)
-        measure(2)
+        flip_weights(1)
         invert_std(1)
+        normalise(1, nc.gpsimd)
+        group_weights(1, nc.scalar.copy)
+        measure(2)
         spread_gains()
-        normalise(1, G)
-        group_weights(0, 1, SC)
-        flip_weights(0, 2, warm=1)
-        measure(3)
+        flip_weights(2)
         invert_std(2)
+        normalise(2, nc.gpsimd)
         flip_h(0)
-        group_weights(0, 2, VC)
-        normalise(2, G)
-        scale_h(0, 0, S)
-        flip_weights(0, 3)
-        scale_h(0, 1, S)
-        flip_weights(1, 0)
+        flip_weights(3)
+        measure(3)
+        group_weights(2, nc.vector.tensor_copy)
+        scale_h(0)
+        flip_weights(4)
         invert_std(3)
+        normalise(3, nc.vector)
         flip_h(1)
-        normalise(3, V)
-        scale_h(1, 0, S)
-        flip_weights(1, 1)
-        group_weights(0, 3, VC)
-        scale_h(1, 1, S)
+        group_weights(3, nc.vector.tensor_copy)
+        scale_h(1)
+        flip_weights(5)
         flip_h(2)
-        regroup_h(0, V)
-        group_weights(1, 0, SC)
-        flip_weights(1, 2)
-        quantise_weights(0, (0,))
-        scale_h(2, 0, S)
-        flip_h(3)
-        quantise_weights(0, (1,))
-        scale_h(2, 1, S)
-        flip_weights(1, 3)
+        group_weights(4, nc.scalar.copy)
+        regroup_h(0)
+        quantise_weights(0)
         quantise_h(0)
-        scale_h(3, 0, S)
-        multiply(0, 0)
-        regroup_h(1, V)
-        scale_h(3, 1, S)
-        group_weights(1, 1, VC)
-        group_weights(1, 2, SC)
+        scale_h(2)
+        flip_weights(6)
+        flip_h(3)
+        regroup_h(1)
         quantise_h(1)
-        group_weights(1, 3, SC)
-        multiply(0, 1)
-        regroup_h(2, V)
-        flip_weights(2, 0)
-        regroup_h(3, V)
-        group_weights(2, 0, SC)
-        flip_weights(2, 1)
+        scale_h(3)
+        flip_weights(7)
+        regroup_h(2)
+        regroup_h(3)
         quantise_h(2)
-        group_weights(2, 1, SC)
-        multiply(0, 2)
         quantise_h(3)
-        gather_pairs(3, 0, SC)
-        multiply(0, 3)
-        finish(0, 0)
-        gather_pairs(3, 1, SC)
-        flip_weights(2, 2)
-        quantise_weights(1, (0,))
-        group_weights(2, 2, SC)
-        flip_weights(2, 3)
-        finish(0, 1)
-        group_weights(2, 3, SC)
-        quantise_weights(1, (1,))
-        gather_pairs(3, 2, SC)
-        multiply(1, 0)
-        finish(0, 2)
-        gather_pairs(3, 3, SC)
-        multiply(1, 1)
-        finish(0, 3)
-        flip_weights(3, 0)
-        finish(1, 0)
-        group_weights(3, 0, SC)
-        flip_weights(3, 1)
-        finish(1, 1)
-        group_weights(3, 1, SC)
-        multiply(1, 2)
-        quantise_weights(2, (0,))
-        gather_pairs(4, 0, SC)
-        multiply(1, 3)
-        quantise_weights(2, (1,))
-        gather_pairs(4, 1, SC)
-        flip_weights(3, 2)
-        finish(1, 2)
-        group_weights(3, 2, SC)
-        flip_weights(3, 3)
-        finish(1, 3)
-        group_weights(3, 3, SC)
-        multiply(2, 0)
-        finish(2, 0)
-        gather_pairs(4, 2, SC)
-        multiply(2, 1)
-        finish(2, 1)
-        gather_pairs(4, 3, SC)
-        flip_weights(4, 0)
-        quantise_weights(3, (0,))
-        group_weights(4, 0, SC)
-        flip_weights(4, 1)
-        quantise_weights(3, (1,))
-        group_weights(4, 1, SC)
-        multiply(2, 2)
-        finish(2, 2)
-        gather_pairs(5, 0, SC)
-        multiply(2, 3)
-        finish(2, 3)
-        flip_weights(4, 2)
-        group_weights(4, 2, SC)
-        flip_weights(4, 3)
-        group_weights(4, 3, SC)
-        multiply(3, 0)
-        finish(3, 0)
-        gather_pairs(5, 2, SC)
-        multiply(3, 1)
-        finish(3, 1)
-        flip_weights(5, 0)
-        quantise_weights(4, (0,))
-        group_weights(5, 0, SC)
-        flip_weights(5, 1)
-        quantise_weights(4, (1,))
-        group_weights(5, 1, SC)
-        multiply(3, 2)
-        finish(3, 2)
-        multiply(3, 3)
-        finish(3, 3)
-        flip_weights(5, 2)
-        group_weights(5, 2, SC)
-        flip_weights(5, 3)
-        group_weights(5, 3, SC)
-        multiply(4, 0)
-        finish(4, 0)
-        multiply(4, 1)
-        quantise_weights(5, (0,))
-        multiply(4, 2)
-        quantise_weights(5, (1,))
-        multiply(4, 3)
-        finish(4, 1)
-        multiply(5, 0)
-        finish(4, 2)
-        multiply(5, 1)
-        finish(4, 3)
-        multiply(5, 2)
-        finish(5, 0)
-        multiply(5, 3)
-        finish(5, 1)
-        finish(5, 2)
-        finish(5, 3)
+        for k in range(5, EARLY * ROW_TILES):
+            group_weights(k, nc.scalar.copy)
+
+        products = [(c, i) for c in range(CHUNKS) for i in range(TOKEN_TILES)]
+        for step in range(len(products) // STEP):
+            first = EARLY * ROW_TILES + (step - 1) * STEP
+            arrivals = [k for k in range(first, first + STEP) if step > 0 and k < W_TILES]
+            for k in arrivals:
+                flip_weights(k)
+            for k in arrivals:
+                group_weights(k, nc.scalar.copy)
+                if GATHERED * ROW_TILES <= k + GATHER_LEAD < W_TILES:
+                    gather_words(k + GATHER_LEAD)
+            pair = products[step * STEP : (step + 1) * STEP]
+            for c, i in pair:
+                multiply(c, i)
+            for c, i in pair:
+                finish(c, i)
+            if step % 2 == 0 and step // 2 + 1 < CHUNKS:
+                quantise_weights(step // 2 + 1)

@@ -30,9 +30,9 @@ ROW_TILES = CHUNK // P
 W_TILES = CHUNKS * ROW_TILES
 
 EARLY = 2
-LOAD_TILES = 2
+HALF_CHUNK = ROW_TILES // 2
 STEP = 2
-GATHERED = 3
+GATHERED = list(range(3 * ROW_TILES, 5 * ROW_TILES)) + list(range(5 * ROW_TILES, W_TILES, 2))
 GATHER_LEAD = ROW_TILES
 
 BN_WIDTH = 512
@@ -68,11 +68,11 @@ def tile_block_pa_kernel(tc, x, W_qkv, b_qkv, g1, beta1, out_0, out_1, out_2):
         w_sb = keep.tile([P, W_TILES, D], BF16)
         bias_all = keep.tile([P, FEATURES], BF16)
 
-        def load_weights(first, last):
-            for k in range(first, last, LOAD_TILES):
+        def load_weights(c, tiles):
+            for k in range(c * ROW_TILES, (c + 1) * ROW_TILES, tiles):
                 nc.sync.dma_start(
-                    out=w_sb[:, k : k + LOAD_TILES, :],
-                    in_=W_qkv[k * P : (k + LOAD_TILES) * P, :].rearrange("(r p) k -> p r k", p=P),
+                    out=w_sb[:, k : k + tiles, :],
+                    in_=W_qkv[k * P : (k + tiles) * P, :].rearrange("(r p) k -> p r k", p=P),
                 )
 
         def load_bias(first, last):
@@ -82,11 +82,15 @@ def tile_block_pa_kernel(tc, x, W_qkv, b_qkv, g1, beta1, out_0, out_1, out_2):
 
         for i in range(TOKEN_TILES):
             rows = slice(i * P, (i + 1) * P)
-            nc.sync.dma_start(out=x_sb[:, i, :], in_=x_rows[rows, :])
+            parts = D // BN_WIDTH if i == 0 else 1
+            for s in range(parts):
+                columns = slice(s * D // parts, (s + 1) * D // parts)
+                nc.sync.dma_start(out=x_sb[:, i, columns], in_=x_rows[rows, columns])
             nc.sync.dma_start(out=w_sb[:, i, :], in_=W_qkv[rows, :])
-        load_weights(ROW_TILES, 3 * ROW_TILES)
+        load_weights(1, HALF_CHUNK)
         load_bias(0, 2 * CHUNK)
-        load_weights(3 * ROW_TILES, W_TILES)
+        for c in range(2, CHUNKS):
+            load_weights(c, ROW_TILES)
         load_bias(2 * CHUNK, FEATURES)
         w_words = w_sb[:].bitcast(F32)
 
@@ -205,8 +209,12 @@ def tile_block_pa_kernel(tc, x, W_qkv, b_qkv, g1, beta1, out_0, out_1, out_2):
             )
             gathered[k] = words
 
-        def flip_weights(k):
+        def flip_weights(k, warm=0):
             flipped = flip_banks.tile([P, PASSES, PAIRS, P], F32, tag="flip", name="w_flipped")
+            for unread in range(warm):
+                nc.tensor.matmul(
+                    out=flipped[:, 0, 0, :], lhsT=ident[:], rhs=ident[:], start=True, stop=True
+                )
             for g in range(PASSES):
                 for u in range(PAIRS):
                     if k in gathered:
@@ -266,18 +274,18 @@ def tile_block_pa_kernel(tc, x, W_qkv, b_qkv, g1, beta1, out_0, out_1, out_2):
             )
 
         measure(0)
-        flip_weights(0)
+        flip_weights(0, warm=5)
         invert_std(0)
         normalise(0, nc.gpsimd)
         group_weights(0, nc.scalar.copy)
         measure(1)
-        flip_weights(1)
+        flip_weights(1, warm=2)
         invert_std(1)
         normalise(1, nc.gpsimd)
         group_weights(1, nc.scalar.copy)
         measure(2)
         spread_gains()
-        flip_weights(2)
+        flip_weights(2, warm=1)
         invert_std(2)
         normalise(2, nc.gpsimd)
         flip_h(0)
@@ -301,6 +309,7 @@ def tile_block_pa_kernel(tc, x, W_qkv, b_qkv, g1, beta1, out_0, out_1, out_2):
         flip_weights(6)
         flip_h(3)
         regroup_h(1)
+        group_weights(5, nc.vector.tensor_copy)
         quantise_h(1)
         scale_h(3)
         flip_weights(7)
@@ -308,7 +317,7 @@ def tile_block_pa_kernel(tc, x, W_qkv, b_qkv, g1, beta1, out_0, out_1, out_2):
         regroup_h(3)
         quantise_h(2)
         quantise_h(3)
-        for k in range(5, EARLY * ROW_TILES):
+        for k in range(6, EARLY * ROW_TILES):
             group_weights(k, nc.scalar.copy)
 
         products = [(c, i) for c in range(CHUNKS) for i in range(TOKEN_TILES)]
@@ -319,7 +328,7 @@ def tile_block_pa_kernel(tc, x, W_qkv, b_qkv, g1, beta1, out_0, out_1, out_2):
                 flip_weights(k)
             for k in arrivals:
                 group_weights(k, nc.scalar.copy)
-                if GATHERED * ROW_TILES <= k + GATHER_LEAD < W_TILES:
+                if k + GATHER_LEAD in GATHERED:
                     gather_words(k + GATHER_LEAD)
             pair = products[step * STEP : (step + 1) * STEP]
             for c, i in pair:

@@ -30,7 +30,7 @@ ROW_TILES = CHUNK // P
 W_TILES = CHUNKS * ROW_TILES
 
 EARLY = 2
-HALF_CHUNK = ROW_TILES // 2
+TWIN = 2
 STEP = 2
 GATHERED = list(range(3 * ROW_TILES, 5 * ROW_TILES)) + list(range(5 * ROW_TILES, W_TILES, 2))
 GATHER_LEAD = ROW_TILES
@@ -68,12 +68,10 @@ def tile_block_pa_kernel(tc, x, W_qkv, b_qkv, g1, beta1, out_0, out_1, out_2):
         w_sb = keep.tile([P, W_TILES, D], BF16)
         bias_all = keep.tile([P, FEATURES], BF16)
 
-        def load_weights(c, tiles):
-            for k in range(c * ROW_TILES, (c + 1) * ROW_TILES, tiles):
-                nc.sync.dma_start(
-                    out=w_sb[:, k : k + tiles, :],
-                    in_=W_qkv[k * P : (k + tiles) * P, :].rearrange("(r p) k -> p r k", p=P),
-                )
+        w_rows = [
+            W_qkv[m * TWIN * P : (m + 1) * TWIN * P, :].rearrange("(p r) k -> p r k", r=TWIN)
+            for m in range(W_TILES // TWIN)
+        ]
 
         def load_bias(first, last):
             nc.sync.dma_start(
@@ -82,15 +80,12 @@ def tile_block_pa_kernel(tc, x, W_qkv, b_qkv, g1, beta1, out_0, out_1, out_2):
 
         for i in range(TOKEN_TILES):
             rows = slice(i * P, (i + 1) * P)
-            parts = D // BN_WIDTH if i == 0 else 1
-            for s in range(parts):
-                columns = slice(s * D // parts, (s + 1) * D // parts)
-                nc.sync.dma_start(out=x_sb[:, i, columns], in_=x_rows[rows, columns])
-            nc.sync.dma_start(out=w_sb[:, i, :], in_=W_qkv[rows, :])
-        load_weights(1, HALF_CHUNK)
-        load_bias(0, 2 * CHUNK)
-        for c in range(2, CHUNKS):
-            load_weights(c, ROW_TILES)
+            nc.sync.dma_start(out=x_sb[:, i, :], in_=x_rows[rows, :])
+            nc.sync.dma_start(out=w_sb[:, i, :], in_=w_rows[i // TWIN][:, i % TWIN, :])
+        for twin in range(ROW_TILES // TWIN, W_TILES // TWIN):
+            if twin == 2 * ROW_TILES // TWIN:
+                load_bias(0, 2 * CHUNK)
+            nc.sync.dma_start(out=w_sb[:, twin * TWIN : (twin + 1) * TWIN, :], in_=w_rows[twin])
         load_bias(2 * CHUNK, FEATURES)
         w_words = w_sb[:].bitcast(F32)
 
@@ -262,10 +257,11 @@ def tile_block_pa_kernel(tc, x, W_qkv, b_qkv, g1, beta1, out_0, out_1, out_2):
         def finish(c, i):
             first = c * CHUNK
             result = results.tile([P, CHUNK], F32)
+            bias = bias_all[:, first : first + CHUNK]
             nc.vector.tensor_tensor(
-                out=result[:],
-                in0=sums[c, i][:],
-                in1=bias_all[:, first : first + CHUNK],
+                out=result[:].rearrange("q (m p r) -> q m p r", r=TWIN, p=P),
+                in0=sums[c, i][:].rearrange("q (m r p) -> q m p r", r=TWIN, p=P),
+                in1=bias.rearrange("q (m p r) -> q m p r", r=TWIN, p=P),
                 op=ALU.add,
             )
             nc.sync.dma_start(

from contextlib import ExitStack

import concourse.mybir as mybir
from concourse.masks import make_identity

F32 = mybir.dt.float32
BF16 = mybir.dt.bfloat16
U32 = mybir.dt.uint32
U8 = mybir.dt.uint8
FP8X4 = mybir.dt.float8_e4m3fn_x4
ACT = mybir.ActivationFunctionType
ALU = mybir.AluOpType

P = 128
TOKENS = 512
D = 1024
FEATURES = 3 * D
LN_EPS = 1e-6

PACK = 4
K_PASS = P * PACK
PASSES = D // K_PASS
PAIR = 2
PAIRS = PACK // PAIR

TOKEN_TILES = TOKENS // P
CHUNK = 512
CHUNKS = FEATURES // CHUNK
ROW_TILES = CHUNK // P
W_TILES = CHUNKS * ROW_TILES

EARLY = 2
TWIN = 2
STEP = 2
GATHERED = list(range(3 * ROW_TILES, 5 * ROW_TILES)) + list(range(5 * ROW_TILES, W_TILES, 2))
GATHER_LEAD = ROW_TILES

BN_WIDTH = 512
BN_OUT = 6

FLOPS = 2 * TOKENS * D * FEATURES


def tile_block_pa_kernel(tc, x, W_qkv, b_qkv, g1, beta1, out_0, out_1, out_2):
    nc = tc.nc
    x_rows = x.flatten_outer_dims()
    out_rows = [o.rearrange("b t h d -> (b t) (h d)") for o in (out_0, out_1, out_2)]

    with ExitStack() as ctx:
        keep = ctx.enter_context(tc.tile_pool(name="keep", bufs=1))
        small = ctx.enter_context(tc.tile_pool(name="small", bufs=TOKEN_TILES))
        normed = ctx.enter_context(tc.tile_pool(name="normed", bufs=TOKEN_TILES))
        grouped = ctx.enter_context(tc.tile_pool(name="grouped", bufs=CHUNKS))
        gathers = ctx.enter_context(tc.tile_pool(name="gathers", bufs=2 * GATHER_LEAD))
        results = ctx.enter_context(tc.tile_pool(name="results", bufs=12))
        flip_banks = ctx.enter_context(tc.psum_pool(name="flip_banks", bufs=4))
        sum_banks = ctx.enter_context(tc.psum_pool(name="sum_banks", bufs=4))
        ctx.enter_context(tc.manual_schedule())

        vectors = keep.tile([P, K_PASS], BF16)
        nc.vector.memset(vectors[:].bitcast(U32), 0)
        for row, vector in ((0, g1), (PASSES, beta1)):
            nc.scalar.dma_start(
                out=vectors[row : row + PASSES, :], in_=vector.rearrange("(r c) -> r c", c=K_PASS)
            )

        x_sb = keep.tile([P, TOKEN_TILES, D], BF16)
        w_sb = keep.tile([P, W_TILES, D], BF16)
        bias_all = keep.tile([P, FEATURES], BF16)

        w_rows = [
            W_qkv[m * TWIN * P : (m + 1) * TWIN * P, :].rearrange("(p r) k -> p r k", r=TWIN)
            for m in range(W_TILES // TWIN)
        ]

        def load_bias(first, last):
            nc.sync.dma_start(
                out=bias_all[:, first:last], in_=b_qkv[first:last].partition_broadcast(P)
            )

        for i in range(TOKEN_TILES):
            rows = slice(i * P, (i + 1) * P)
            nc.sync.dma_start(out=x_sb[:, i, :], in_=x_rows[rows, :])
            nc.sync.dma_start(out=w_sb[:, i, :], in_=w_rows[i // TWIN][:, i % TWIN, :])
        for twin in range(ROW_TILES // TWIN, W_TILES // TWIN):
            if twin == 2 * ROW_TILES // TWIN:
                load_bias(0, 2 * CHUNK)
            nc.sync.dma_start(out=w_sb[:, twin * TWIN : (twin + 1) * TWIN, :], in_=w_rows[twin])
        load_bias(2 * CHUNK, FEATURES)
        w_words = w_sb[:].bitcast(F32)

        eps_col = keep.tile([P, 1], F32)
        nc.vector.memset(eps_col[:], LN_EPS)
        table_warmer = keep.tile([P, 1], F32)
        nc.scalar.activation(out=table_warmer[:], in_=eps_col[:], func=ACT.Abs_reciprocal_sqrt)
        ident = keep.tile([P, P], F32)
        make_identity(nc, ident[:])

        h_codes = keep.tile([P, TOKEN_TILES, PASSES, P], U32, align_bytes=64)
        h_scales = keep.tile([P, TOKEN_TILES, PASSES, P], U8, align_bytes=64)
        w_codes = keep.tile([P, CHUNKS, PASSES, CHUNK], U32, align_bytes=64)
        w_scales = keep.tile([P, CHUNKS, PASSES, CHUNK], U8, align_bytes=64)
        h_planes = keep.tile([P, TOKEN_TILES, PASSES, PACK, P], BF16)
        h_grouped = keep.tile([P, TOKEN_TILES, PASSES, P, PACK], BF16, align_bytes=64)
        gain_cols = keep.tile([P, 2 * PASSES * PACK], F32)
        beta_at = PASSES * PACK

        mean_vars, rstds, xns, h_banks = {}, {}, {}, {}
        gathered, w_banks, w_grouped, sums = {}, {}, {}, {}

        def spread_gains():
            flipped = flip_banks.tile([P, PAIRS, P], F32, tag="flip", name="gain_flipped")
            for u in range(PAIRS):
                nc.tensor.transpose(
                    flipped[:, u, :], vectors[:].bitcast(F32)[:, u::PAIRS], ident[:]
                )
            pairs = keep.tile([P, 2 * PASSES * PAIRS], F32)
            nc.vector.tensor_copy(
                out=pairs[:].rearrange("p (r u) -> p r u", u=PAIRS),
                in_=flipped[:, :, 0 : 2 * PASSES].rearrange("p u r -> p r u"),
            )
            nc.vector.tensor_copy(out=gain_cols[:], in_=pairs[:].bitcast(BF16))

        def measure(i):
            stats = small.tile([P, D // BN_WIDTH, BN_OUT], F32)
            for s in range(D // BN_WIDTH):
                nc.vector.bn_stats(
                    out=stats[:, s, :], in_=x_sb[:, i, s * BN_WIDTH : (s + 1) * BN_WIDTH]
                )
            mean_var = small.tile([P, 2], F32)
            nc.vector.bn_aggr(out=mean_var[:], in_=stats[:].rearrange("p s d -> p (s d)"))
            mean_vars[i] = mean_var

        def invert_std(i):
            rstd = small.tile([P, 1], F32)
            nc.scalar.activation(
                out=rstd[:],
                in_=mean_vars[i][:, 1:2],
                func=ACT.Abs_reciprocal_sqrt,
                bias=eps_col[:],
            )
            rstds[i] = rstd

        def normalise(i, engine):
            neg_mean = small.tile([P, 1], F32)
            engine.tensor_scalar(
                out=neg_mean[:],
                in0=mean_vars[i][:, 0:1],
                scalar1=-1.0,
                scalar2=0.0,
                op0=ALU.mult,
                op1=ALU.add,
            )
            xn = normed.tile([P, PACK, D // PACK], F32)
            engine.tensor_scalar(
                out=xn[:],
                in0=x_sb[:, i, :].rearrange("p (j t) -> p t j", t=PACK),
                scalar1=neg_mean[:],
                scalar2=rstds[i][:],
                op0=ALU.add,
                op1=ALU.mult,
            )
            xns[i] = xn

        def flip_h(i):
            for g in range(PASSES):
                flipped = sum_banks.tile([P, PACK, P], F32, tag="sum", name="h_flipped")
                for t in range(PACK):
                    nc.tensor.transpose(
                        flipped[:, t, :], xns[i][:, t, g * P : (g + 1) * P], ident[:]
                    )
                h_banks[i, g] = flipped

        def scale_h(i):
            for g in range(PASSES):
                for t in range(PACK):
                    col = PACK * g + t
                    nc.scalar.activation(
                        out=h_planes[:, i, g, t, :],
                        in_=h_banks[i, g][:, t, :],
                        func=ACT.Identity,
                        scale=gain_cols[:, col : col + 1],
                        bias=gain_cols[:, beta_at + col : beta_at + col + 1],
                    )

        def regroup_h(i):
            nc.vector.tensor_copy(
                out=h_grouped[:, i, :, :, :],
                in_=h_planes[:, i, :, :, :].rearrange("p g t n -> p g n t"),
            )

        def quantise_h(i):
            nc.vector.quantize_mx(
                out=h_codes[:, i, :, :].rearrange("p g n -> p (g n)").bitcast(FP8X4),
                scales=h_scales[:, i, :, :].rearrange("p g n -> p (g n)"),
                in_=h_grouped[:, i, :, :, :].rearrange("p g n t -> p (g n t)"),
            )

        def gather_words(k):
            words = gathers.tile([P, PASSES, PAIRS, P], F32)
            nc.scalar.copy(
                out=words[:].rearrange("p g u j -> p g j u"),
                in_=w_words[:, k, :].rearrange("p (g j u) -> p g j u", g=PASSES, u=PAIRS),
            )
            gathered[k] = words

        def flip_weights(k, warm=0):
            flipped = flip_banks.tile([P, PASSES, PAIRS, P], F32, tag="flip", name="w_flipped")
            for unread in range(warm):
                nc.tensor.matmul(
                    out=flipped[:, 0, 0, :], lhsT=ident[:], rhs=ident[:], start=True, stop=True
                )
            for g in range(PASSES):
                for u in range(PAIRS):
                    if k in gathered:
                        pairs = gathered[k][:, g, u, :]
                    else:
                        first = g * PAIRS * P + u
                        pairs = w_words[:, k, first : (g + 1) * PAIRS * P : PAIRS]
                    nc.tensor.transpose(flipped[:, g, u, :], pairs, ident[:])
            w_banks[k] = flipped

        def group_weights(k, copy):
            c, r = divmod(k, ROW_TILES)
            if r == 0:
                w_grouped[c] = grouped.tile(
                    [P, PASSES, CHUNK * PACK], BF16, align_bytes=64, name="w_grouped"
                )
            words = w_grouped[c][:].bitcast(F32).rearrange("p g (f u) -> p g f u", u=PAIRS)
            copy(
                out=words[:, :, r * P : (r + 1) * P, :],
                in_=w_banks[k][:].rearrange("p g u f -> p g f u"),
            )

        def quantise_weights(c):
            for g in range(PASSES):
                nc.vector.quantize_mx(
                    out=w_codes[:, c, g, :].bitcast(FP8X4),
                    scales=w_scales[:, c, g, :],
                    in_=w_grouped[c][:, g, :],
                )

        def multiply(c, i):
            bank = sum_banks.tile([P, CHUNK], F32, tag="sum", name="sums")
            for g in range(PASSES):
                nc.tensor.matmul_mx(
                    out=bank[:],
                    lhsT=h_codes[:, i, g, :].bitcast(FP8X4),
                    lhsT_scale=h_scales[:, i, g, :],
                    rhs=w_codes[:, c, g, :].bitcast(FP8X4),
                    rhs_scale=w_scales[:, c, g, :],
                    start=(g == 0),
                    stop=(g == PASSES - 1),
                )
            sums[c, i] = bank

        def finish(c, i):
            first = c * CHUNK
            result = results.tile([P, CHUNK], F32)
            bias = bias_all[:, first : first + CHUNK]
            nc.vector.tensor_tensor(
                out=result[:].rearrange("q (m p r) -> q m p r", r=TWIN, p=P),
                in0=sums[c, i][:].rearrange("q (m r p) -> q m p r", r=TWIN, p=P),
                in1=bias.rearrange("q (m p r) -> q m p r", r=TWIN, p=P),
                op=ALU.add,
            )
            nc.sync.dma_start(
                out=out_rows[first // D][i * P : (i + 1) * P, first % D : first % D + CHUNK],
                in_=result[:],
            )

        measure(0)
        flip_weights(0, warm=5)
        invert_std(0)
        normalise(0, nc.gpsimd)
        group_weights(0, nc.scalar.copy)
        measure(1)
        flip_weights(1, warm=2)
        invert_std(1)
        normalise(1, nc.gpsimd)
        group_weights(1, nc.scalar.copy)
        measure(2)
        spread_gains()
        flip_weights(2, warm=1)
        invert_std(2)
        normalise(2, nc.gpsimd)
        flip_h(0)
        flip_weights(3)
        measure(3)
        group_weights(2, nc.vector.tensor_copy)
        scale_h(0)
        flip_weights(4)
        invert_std(3)
        normalise(3, nc.vector)
        flip_h(1)
        group_weights(3, nc.vector.tensor_copy)
        scale_h(1)
        flip_weights(5)
        flip_h(2)
        group_weights(4, nc.scalar.copy)
        regroup_h(0)
        quantise_weights(0)
        quantise_h(0)
        scale_h(2)
        flip_weights(6)
        flip_h(3)
        regroup_h(1)
        group_weights(5, nc.vector.tensor_copy)
        quantise_h(1)
        scale_h(3)
        flip_weights(7)
        regroup_h(2)
        regroup_h(3)
        quantise_h(2)
        quantise_h(3)
        for k in range(6, EARLY * ROW_TILES):
            group_weights(k, nc.scalar.copy)

        products = [(c, i) for c in range(CHUNKS) for i in range(TOKEN_TILES)]
        for step in range(len(products) // STEP):
            first = EARLY * ROW_TILES + (step - 1) * STEP
            arrivals = [k for k in range(first, first + STEP) if step > 0 and k < W_TILES]
            for k in arrivals:
                flip_weights(k)
            for k in arrivals:
                group_weights(k, nc.scalar.copy)
                if k + GATHER_LEAD in GATHERED:
                    gather_words(k + GATHER_LEAD)
            pair = products[step * STEP : (step + 1) * STEP]
            for c, i in pair:
                multiply(c, i)
            for c, i in pair:
                finish(c, i)
            if step % 2 == 0 and step // 2 + 1 < CHUNKS:
                quantise_weights(step // 2 + 1)
